import numpy as np
import ml_dtypes


def mxq(x, axis, fmt="e4m3"):
    dtype, down = {"e4m3": (ml_dtypes.float8_e4m3fn, 7), "e5m2": (ml_dtypes.float8_e5m2, 14)}[fmt]
    v = np.moveaxis(np.asarray(x, np.float32).astype(ml_dtypes.bfloat16).astype(np.float64), axis, -1)
    blocks = v.reshape(v.shape[:-1] + (-1, 32))
    amax = np.abs(blocks).max(-1, keepdims=True)
    byte = np.maximum(np.where(amax > 0, np.frexp(amax)[1] - 1 + 127, 0) - down, 1)
    scale = np.exp2(byte - 127.0)
    codes = (blocks / scale).astype(np.float32).astype(dtype).astype(np.float64)
    return np.moveaxis((codes * scale).reshape(v.shape), -1, axis)


WIDE = False


def mx_kscale(k):
    if not WIDE:
        return np.ones(k)
    levels = np.array([10, -10, 5, -5, 0])
    a = np.random.permutation(np.resize(levels, k // 512 * 4)).reshape(k // 512, 4)
    idx = np.arange(k)
    return np.exp2(a[idx // 512, idx % 128 // 32])


BF16 = ml_dtypes.bfloat16


def bf(x):
    return np.asarray(x, np.float32).astype(BF16)


def f64(x):
    return np.asarray(x).astype(np.float64)


E2M1 = np.array([0.0, 0.5, 1.0, 1.5, 2.0, 3.0, 4.0, 6.0, -0.0, -0.5, -1.0, -1.5, -2.0, -3.0, -4.0, -6.0])


def pack_weight(w, fmt):
    k, n = w.shape
    w = f64(bf(w)).reshape(k // 32, 32, n)
    amax = np.abs(w).max(1)
    if fmt == "e4m3":
        byte = np.frexp(amax)[1] - 1 + 127 - 7
    else:
        mant, ex = np.frexp(amax / 6.0)
        byte = np.where(mant > 0.5, ex, ex - 1) + 127
    byte = np.clip(np.where(amax > 0, byte, 1), 1, 254)
    scaled = (w * np.exp2(127.0 - byte)[:, None, :]).reshape(k, n).astype(np.float32)
    by_word = np.ascontiguousarray(scaled.reshape(k // 512, 128, 4, n).transpose(0, 1, 3, 2))
    if fmt == "e4m3":
        words = by_word.astype(ml_dtypes.float8_e4m3fn).view(np.uint8)
    else:
        c = by_word.astype(ml_dtypes.float4_e2m1fn).view(np.uint8) & 0xF
        words = c[..., 0::2] | (c[..., 1::2] << 4)
    return np.ascontiguousarray(words), np.ascontiguousarray(byte.astype(np.uint8).reshape(k // 512, 16, n))


def unpack_weight(words, scales, fmt):
    g, p, n, _ = words.shape
    if fmt == "e4m3":
        vals = np.ascontiguousarray(words).view(ml_dtypes.float8_e4m3fn).astype(np.float64)
    else:
        nib = np.empty((g, p, n, 4), np.uint8)
        nib[..., 0::2] = words & 0xF
        nib[..., 1::2] = words >> 4
        vals = E2M1[nib]
    vals = vals * np.repeat(np.exp2(scales.astype(np.float64) - 127.0), 8, axis=1)[..., None]
    return vals.transpose(0, 1, 3, 2).reshape(g * 512, n)


B, T, H, A = 256, 5, 512, 512
FMT = "e4m3"


def softmax_t(z):
    e = np.exp(z - z.max(axis=1, keepdims=True))
    return e / e.sum(axis=1, keepdims=True)


def setup_inputs():
    s = mx_kscale(2 * H)
    ht = bf(np.random.standard_normal((B, H)) * s[:H])
    ct = bf(np.random.standard_normal((B, H)) * s[H:])
    hi = bf(np.random.standard_normal((B, T, H)))
    W_as_words, W_as_scales = pack_weight(np.random.standard_normal((2 * H, A)) * 0.7 / np.sqrt(2 * H) / s[:, None], FMT)
    W_ah_words, W_ah_scales = pack_weight(np.random.standard_normal((H, A)) * 0.7 / np.sqrt(H), FMT)
    ba = bf(np.random.standard_normal((1, A)) * 0.3)
    v = bf(np.random.standard_normal((1, A)) * 0.5)
    W_a_words, W_a_scales = pack_weight(np.random.standard_normal((A, H)) * 2.0 / np.sqrt(A), FMT)
    return {"ht": ht,
            "ct": ct,
            "hi": hi,
            "W_as_words": W_as_words,
            "W_as_scales": W_as_scales,
            "W_ah_words": W_ah_words,
            "W_ah_scales": W_ah_scales,
            "ba": ba,
            "v": v,
            "W_a_words": W_a_words,
            "W_a_scales": W_a_scales}


def reference(ht, ct, hi, W_as_words, W_as_scales, W_ah_words, W_ah_scales, ba, v, W_a_words, W_a_scales):
    hi = f64(hi)
    q = np.concatenate((f64(ht), f64(ct)), axis=-1)
    a_s = mxq(q, 1, "e4m3") @ unpack_weight(W_as_words, W_as_scales, FMT)
    ah = mxq(hi, 2, "e4m3") @ unpack_weight(W_ah_words, W_ah_scales, FMT)
    etk = np.tanh(a_s[:, None, :] + ah + f64(ba))
    etk = mxq(etk, 2, "e4m3") @ unpack_weight(W_a_words, W_a_scales, FMT)
    atk = softmax_t(etk)
    return np.sum(atk * hi, axis=1)

@@ -1,0 +1,224 @@
+from contextlib import ExitStack
+
+import concourse.mybir as mybir
+from concourse.masks import make_identity
+
+F32 = mybir.dt.float32
+BF16 = mybir.dt.bfloat16
+I32 = mybir.dt.int32
+U32 = mybir.dt.uint32
+U8 = mybir.dt.uint8
+FP8X4 = mybir.dt.float8_e4m3fn_x4
+ACT = mybir.ActivationFunctionType
+
+P = 128
+PACK = 4
+B, T, H, A = 256, 5, 512, 512
+B_TILES = B // P
+TOKEN_TILES = B_TILES * T
+LAG = 2
+
+PLANE_W_AS = (0, 4)
+PLANE_W_AH = 8
+PLANE_W_A = 12
+
+FLOPS = 2 * B * (2 * H) * A + 2 * B * T * H * A + 2 * B * T * A * H
+
+
+def load_scale_rows(nc, w_planes, first_row, scales):
+    n_planes = scales.shape[0]
+    for quadrant in range(4):
+        first = 32 * quadrant + first_row
+        nc.sync.dma_start(
+            out=w_planes[first : first + 4 * n_planes, :].bitcast(I32),
+            in_=scales[:, 4 * quadrant : 4 * quadrant + 4, :].bitcast(I32),
+        )
+
+
+def load_words(nc, words_sb, words):
+    nc.sync.dma_start(
+        out=words_sb.bitcast(I32),
+        in_=words.rearrange("p n t -> p (n t)").bitcast(I32),
+    )
+
+
+def tile_haint_attention_kernel(
+    tc,
+    ht,
+    ct,
+    hi,
+    W_as_words,
+    W_as_scales,
+    W_ah_words,
+    W_ah_scales,
+    ba,
+    v,
+    W_a_words,
+    W_a_scales,
+    out,
+):
+    nc = tc.nc
+    with ExitStack() as ctx:
+        keep = ctx.enter_context(tc.tile_pool(name="keep", bufs=1))
+        stage = ctx.enter_context(tc.tile_pool(name="stage", bufs=3))
+        soft = ctx.enter_context(tc.tile_pool(name="soft", bufs=B_TILES))
+        turned = ctx.enter_context(tc.psum_pool(name="turned", bufs=3))
+        sums = ctx.enter_context(tc.psum_pool(name="sums", bufs=1))
+
+        w_planes = keep.tile([P, A], U8, align_bytes=64)
+        nc.vector.memset(w_planes[:].bitcast(I32), 0)
+
+        ht_sb = keep.tile([P, B_TILES, H], BF16)
+        ct_sb = keep.tile([P, B_TILES, H], BF16)
+        nc.sync.dma_start(out=ht_sb[:], in_=ht.rearrange("(c p) k -> p c k", p=P))
+        nc.sync.dma_start(out=ct_sb[:], in_=ct.rearrange("(c p) k -> p c k", p=P))
+        hi_sb = [keep.tile([P, T, H], BF16, name="hi_sb%d" % c) for c in range(B_TILES)]
+        nc.sync.dma_start(out=hi_sb[0][:], in_=hi[0:P])
+
+        load_scale_rows(nc, w_planes, PLANE_W_AS[0], W_as_scales)
+        load_scale_rows(nc, w_planes, PLANE_W_AH, W_ah_scales)
+        w_as = keep.tile([P, 2, A], U32, align_bytes=64)
+        w_ah = keep.tile([P, A], U32, align_bytes=64)
+        w_a = keep.tile([P, H], U32, align_bytes=64)
+        load_words(nc, w_as[:, 0, :], W_as_words[0])
+        load_words(nc, w_as[:, 1, :], W_as_words[1])
+        load_words(nc, w_ah[:], W_ah_words[0])
+        ba_all = keep.tile([P, A], BF16)
+        nc.sync.dma_start(out=ba_all[:], in_=ba.rearrange("o a -> (o a)").partition_broadcast(P))
+        nc.sync.dma_start(out=hi_sb[1][:], in_=hi[P : 2 * P])
+        load_scale_rows(nc, w_planes, PLANE_W_A, W_a_scales)
+        load_words(nc, w_a[:], W_a_words[0])
+
+        ident_f32 = keep.tile([P, P], F32)
+        ident_bf16 = keep.tile([P, P], BF16)
+        make_identity(nc, ident_f32[:])
+        make_identity(nc, ident_bf16[:])
+
+        q_codes = keep.tile([P, 2 * B_TILES, P], U32, align_bytes=64)
+        q_planes = keep.tile([P, 2 * B_TILES, P], U8, align_bytes=64)
+        hi_codes = keep.tile([P, TOKEN_TILES, P], U32, align_bytes=64)
+        hi_planes = keep.tile([P, TOKEN_TILES, P], U8, align_bytes=64)
+        g_codes = keep.tile([P, TOKEN_TILES, P], U32, align_bytes=64)
+        g_planes = keep.tile([P, TOKEN_TILES, P], U8, align_bytes=64)
+
+        def quantise_two_inputs(sources, codes, planes):
+            words_t = turned.tile([P, 2, 2, P], F32, tag="turned")
+            for o in range(2):
+                words = sources[o].bitcast(F32)
+                for u in range(2):
+                    nc.tensor.transpose(words_t[:, o, u, :], words[:, u : H // 2 : 2], ident_f32[:])
+            grouped = stage.tile([P, 2, P, PACK], BF16, align_bytes=64)
+            nc.scalar.copy(out=grouped[:].bitcast(F32), in_=words_t[:].rearrange("p o u r -> p o r u"))
+            nc.vector.quantize_mx(
+                out=codes.rearrange("p o r -> p (o r)").bitcast(FP8X4),
+                scales=planes.rearrange("p o r -> p (o r)"),
+                in_=grouped[:].rearrange("p o r j -> p (o r j)"),
+            )
+
+        for c in range(B_TILES):
+            quantise_two_inputs(
+                (ht_sb[:, c, :], ct_sb[:, c, :]),
+                q_codes[:, 2 * c : 2 * c + 2, :],
+                q_planes[:, 2 * c : 2 * c + 2, :],
+            )
+        for pair in range(TOKEN_TILES // 2):
+            tiles = (divmod(2 * pair, T), divmod(2 * pair + 1, T))
+            quantise_two_inputs(
+                [hi_sb[c][:, t, :] for c, t in tiles],
+                hi_codes[:, 2 * pair : 2 * pair + 2, :],
+                hi_planes[:, 2 * pair : 2 * pair + 2, :],
+            )
+
+        as_ba = [keep.tile([P, A], F32, name="as_ba%d" % c) for c in range(B_TILES)]
+        for c in range(B_TILES):
+            a_s = sums.tile([P, A], F32, tag="sums%d" % c)
+            for half in range(2):
+                nc.tensor.matmul_mx(
+                    out=a_s[:],
+                    lhsT=q_codes[:, 2 * c + half, :].bitcast(FP8X4),
+                    lhsT_scale=q_planes[:, 2 * c + half, :],
+                    rhs=w_as[:, half, :].bitcast(FP8X4),
+                    rhs_scale=w_planes[PLANE_W_AS[half] : P, :],
+                    start=(half == 0),
+                    stop=(half == 1),
+                )
+            nc.vector.tensor_add(out=as_ba[c][:], in0=a_s[:], in1=ba_all[:])
+
+        g_rows = {}
+
+        def tanh_of_tile(i):
+            c, t = divmod(i, T)
+            ah = sums.tile([P, A], F32, tag="sums%d" % t)
+            nc.tensor.matmul_mx(
+                out=ah[:],
+                lhsT=hi_codes[:, i, :].bitcast(FP8X4),
+                lhsT_scale=hi_planes[:, i, :],
+                rhs=w_ah[:].bitcast(FP8X4),
+                rhs_scale=w_planes[PLANE_W_AH:P, :],
+                start=True,
+                stop=True,
+            )
+            pre = stage.tile([P, A], F32)
+            nc.vector.tensor_add(out=pre[:], in0=ah[:], in1=as_ba[c][:])
+            g_sb = stage.tile([P, A], BF16, bufs=LAG + 2)
+            nc.scalar.activation(out=g_sb[:], in_=pre[:], func=ACT.Tanh)
+            g_rows[i] = g_sb
+
+        def quantise_g(i):
+            g_t = turned.tile([P, PACK, P], BF16, tag="turned")
+            for j in range(PACK):
+                nc.tensor.transpose(g_t[:, j, :], g_rows[i][:, j:A:PACK], ident_bf16[:])
+            grouped_g = stage.tile([P, P, PACK], BF16, align_bytes=64)
+            nc.scalar.copy(out=grouped_g[:], in_=g_t[:].rearrange("p j r -> p r j"))
+            nc.vector.quantize_mx(
+                out=g_codes[:, i, :].bitcast(FP8X4),
+                scales=g_planes[:, i, :],
+                in_=grouped_g[:].rearrange("p r j -> p (r j)"),
+            )
+
+        for i in range(TOKEN_TILES + LAG):
+            if i < TOKEN_TILES:
+                tanh_of_tile(i)
+            if i >= LAG:
+                quantise_g(i - LAG)
+
+        for c in range(B_TILES):
+            z = []
+            for t in range(T):
+                z_t = sums.tile([P, H], F32, tag="sums%d" % t)
+                nc.tensor.matmul_mx(
+                    out=z_t[:],
+                    lhsT=g_codes[:, c * T + t, :].bitcast(FP8X4),
+                    lhsT_scale=g_planes[:, c * T + t, :],
+                    rhs=w_a[:].bitcast(FP8X4),
+                    rhs_scale=w_planes[PLANE_W_A:P, :],
+                    start=True,
+                    stop=True,
+                )
+                z.append(z_t)
+
+            top = soft.tile([P, H], F32)
+            top_b = soft.tile([P, H], F32)
+            nc.scalar.copy(out=top[:], in_=z[0][:])
+            nc.scalar.copy(out=top_b[:], in_=z[2][:])
+            nc.vector.tensor_max(out=top[:], in0=top[:], in1=z[1][:])
+            nc.vector.tensor_max(out=top_b[:], in0=top_b[:], in1=z[3][:])
+            nc.vector.tensor_max(out=top[:], in0=top[:], in1=z[4][:])
+            nc.vector.tensor_max(out=top[:], in0=top[:], in1=top_b[:])
+
+            terms = soft.tile([P, 2, T, H], F32)
+            for t in range(T):
+                nc.vector.tensor_sub(out=terms[:, 0, t, :], in0=z[t][:], in1=top[:])
+                nc.scalar.activation(out=terms[:, 0, t, :], in_=terms[:, 0, t, :], func=ACT.Exp)
+            for t in range(T):
+                nc.vector.tensor_mul(out=terms[:, 1, t, :], in0=terms[:, 0, t, :], in1=hi_sb[c][:, t, :])
+
+            nc.vector.tensor_add(out=terms[:, :, 0:2, :], in0=terms[:, :, 0:2, :], in1=terms[:, :, 2:4, :])
+            nc.vector.tensor_add(out=terms[:, :, 0, :], in0=terms[:, :, 0, :], in1=terms[:, :, 1, :])
+            nc.vector.tensor_add(out=terms[:, :, 0, :], in0=terms[:, :, 0, :], in1=terms[:, :, 4, :])
+
+            inverse = soft.tile([P, H], F32)
+            nc.vector.reciprocal(out=inverse[:], in_=terms[:, 0, 0, :])
+            pooled = soft.tile([P, H], F32)
+            nc.vector.tensor_mul(out=pooled[:], in0=terms[:, 1, 0, :], in1=inverse[:])
+            nc.sync.dma_start(out=out[c * P : (c + 1) * P, :], in_=pooled[:])

@@ -16,7 +16,12 @@ PACK = 4
 B, T, H, A = 256, 5, 512, 512
 B_TILES = B // P
 TOKEN_TILES = B_TILES * T
-LAG = 2
+H_SLICES = H // P
+Q_INPUTS = 2 * B_TILES
+INPUTS = Q_INPUTS + TOKEN_TILES
+
+TURN_LAG = 1
+QUANT_LAG = 3
 
 PLANE_W_AS = (0, 4)
 PLANE_W_AH = 8
@@ -67,6 +72,8 @@ def tile_haint_attention_kernel(
 
         w_planes = keep.tile([P, A], U8, align_bytes=64)
         nc.vector.memset(w_planes[:].bitcast(I32), 0)
+        ident_f32 = keep.tile([P, P], F32)
+        make_identity(nc, ident_f32[:])
 
         ht_sb = keep.tile([P, B_TILES, H], BF16)
         ct_sb = keep.tile([P, B_TILES, H], BF16)
@@ -89,136 +96,183 @@ def tile_haint_attention_kernel(
         load_scale_rows(nc, w_planes, PLANE_W_A, W_a_scales)
         load_words(nc, w_a[:], W_a_words[0])
 
-        ident_f32 = keep.tile([P, P], F32)
-        ident_bf16 = keep.tile([P, P], BF16)
-        make_identity(nc, ident_f32[:])
-        make_identity(nc, ident_bf16[:])
-
-        q_codes = keep.tile([P, 2 * B_TILES, P], U32, align_bytes=64)
-        q_planes = keep.tile([P, 2 * B_TILES, P], U8, align_bytes=64)
-        hi_codes = keep.tile([P, TOKEN_TILES, P], U32, align_bytes=64)
-        hi_planes = keep.tile([P, TOKEN_TILES, P], U8, align_bytes=64)
+        x_codes = keep.tile([P, INPUTS, P], U32, align_bytes=64)
+        x_planes = keep.tile([P, INPUTS, P], U8, align_bytes=64)
         g_codes = keep.tile([P, TOKEN_TILES, P], U32, align_bytes=64)
         g_planes = keep.tile([P, TOKEN_TILES, P], U8, align_bytes=64)
+        sources = [(ht_sb, ct_sb)[half][:, c, :] for c in range(B_TILES) for half in range(2)]
+        sources.extend([hi_sb[c][:, t, :] for c in range(B_TILES) for t in range(T)])
+        grouped_inputs = {}
 
-        def quantise_two_inputs(sources, codes, planes):
-            words_t = turned.tile([P, 2, 2, P], F32, tag="turned")
-            for o in range(2):
-                words = sources[o].bitcast(F32)
-                for u in range(2):
-                    nc.tensor.transpose(words_t[:, o, u, :], words[:, u : H // 2 : 2], ident_f32[:])
-            grouped = stage.tile([P, 2, P, PACK], BF16, align_bytes=64)
-            nc.scalar.copy(out=grouped[:].bitcast(F32), in_=words_t[:].rearrange("p o u r -> p o r u"))
+        def turn_input(k):
+            words_t = turned.tile([P, 2, P], F32, tag="turned")
+            words = sources[k].bitcast(F32)
+            for u in range(2):
+                nc.tensor.transpose(words_t[:, u, :], words[:, u : H // 2 : 2], ident_f32[:])
+            grouped = stage.tile([P, P, PACK], BF16, align_bytes=64)
+            copy_out = nc.vector.tensor_copy if k < Q_INPUTS else nc.scalar.copy
+            copy_out(out=grouped[:].bitcast(F32), in_=words_t[:].rearrange("p u r -> p r u"))
+            grouped_inputs[k] = grouped
+
+        def quantise_input(k):
             nc.vector.quantize_mx(
-                out=codes.rearrange("p o r -> p (o r)").bitcast(FP8X4),
-                scales=planes.rearrange("p o r -> p (o r)"),
-                in_=grouped[:].rearrange("p o r j -> p (o r j)"),
+                out=x_codes[:, k, :].bitcast(FP8X4),
+                scales=x_planes[:, k, :],
+                in_=grouped_inputs[k][:].rearrange("p r j -> p (r j)"),
             )
 
-        for c in range(B_TILES):
-            quantise_two_inputs(
-                (ht_sb[:, c, :], ct_sb[:, c, :]),
-                q_codes[:, 2 * c : 2 * c + 2, :],
-                q_planes[:, 2 * c : 2 * c + 2, :],
-            )
-        for pair in range(TOKEN_TILES // 2):
-            tiles = (divmod(2 * pair, T), divmod(2 * pair + 1, T))
-            quantise_two_inputs(
-                [hi_sb[c][:, t, :] for c, t in tiles],
-                hi_codes[:, 2 * pair : 2 * pair + 2, :],
-                hi_planes[:, 2 * pair : 2 * pair + 2, :],
-            )
+        first_inputs = Q_INPUTS + T
+        for k in range(first_inputs + 1):
+            if k < first_inputs:
+                turn_input(k)
+            if k > 0:
+                quantise_input(k - 1)
 
-        as_ba = [keep.tile([P, A], F32, name="as_ba%d" % c) for c in range(B_TILES)]
+        as_ba = [keep.tile([P, PACK, P], F32, name="as_ba%d" % c) for c in range(B_TILES)]
         for c in range(B_TILES):
-            a_s = sums.tile([P, A], F32, tag="sums%d" % c)
+            a_s = sums.tile([P, A], F32, tag="sums%d" % (3 + c))
             for half in range(2):
                 nc.tensor.matmul_mx(
                     out=a_s[:],
-                    lhsT=q_codes[:, 2 * c + half, :].bitcast(FP8X4),
-                    lhsT_scale=q_planes[:, 2 * c + half, :],
+                    lhsT=x_codes[:, 2 * c + half, :].bitcast(FP8X4),
+                    lhsT_scale=x_planes[:, 2 * c + half, :],
                     rhs=w_as[:, half, :].bitcast(FP8X4),
                     rhs_scale=w_planes[PLANE_W_AS[half] : P, :],
                     start=(half == 0),
                     stop=(half == 1),
                 )
-            nc.vector.tensor_add(out=as_ba[c][:], in0=a_s[:], in1=ba_all[:])
+            nc.vector.tensor_add(
+                out=as_ba[c][:],
+                in0=a_s[:].rearrange("p (r j) -> p j r", j=PACK),
+                in1=ba_all[:].rearrange("p (r j) -> p j r", j=PACK),
+            )
 
-        g_rows = {}
+        pre_of = {}
+        grouped_g_of = {}
 
-        def tanh_of_tile(i):
-            c, t = divmod(i, T)
-            ah = sums.tile([P, A], F32, tag="sums%d" % t)
+        def add_of_tile(i):
+            ah = sums.tile([P, A], F32, tag="sums%d" % (3 + i % 2))
             nc.tensor.matmul_mx(
                 out=ah[:],
-                lhsT=hi_codes[:, i, :].bitcast(FP8X4),
-                lhsT_scale=hi_planes[:, i, :],
+                lhsT=x_codes[:, Q_INPUTS + i, :].bitcast(FP8X4),
+                lhsT_scale=x_planes[:, Q_INPUTS + i, :],
                 rhs=w_ah[:].bitcast(FP8X4),
                 rhs_scale=w_planes[PLANE_W_AH:P, :],
                 start=True,
                 stop=True,
             )
-            pre = stage.tile([P, A], F32)
-            nc.vector.tensor_add(out=pre[:], in0=ah[:], in1=as_ba[c][:])
-            g_sb = stage.tile([P, A], BF16, bufs=LAG + 2)
-            nc.scalar.activation(out=g_sb[:], in_=pre[:], func=ACT.Tanh)
-            g_rows[i] = g_sb
+            pre = stage.tile([P, PACK, P], F32)
+            nc.vector.tensor_add(out=pre[:], in0=ah[:].rearrange("p (r j) -> p j r", j=PACK), in1=as_ba[i // T][:])
+            pre_of[i] = pre
+
+        def tanh_of_tile(i):
+            pre_t = turned.tile([P, PACK, P], F32, tag="turned")
+            for j in range(PACK):
+                nc.tensor.transpose(pre_t[:, j, :], pre_of[i][:, j, :], ident_f32[:])
+            grouped_g = stage.tile([P, P, PACK], BF16, align_bytes=64, bufs=QUANT_LAG + 1)
+            nc.scalar.activation(out=grouped_g[:], in_=pre_t[:].rearrange("p j r -> p r j"), func=ACT.Tanh)
+            grouped_g_of[i] = grouped_g
 
         def quantise_g(i):
-            g_t = turned.tile([P, PACK, P], BF16, tag="turned")
-            for j in range(PACK):
-                nc.tensor.transpose(g_t[:, j, :], g_rows[i][:, j:A:PACK], ident_bf16[:])
-            grouped_g = stage.tile([P, P, PACK], BF16, align_bytes=64)
-            nc.scalar.copy(out=grouped_g[:], in_=g_t[:].rearrange("p j r -> p r j"))
             nc.vector.quantize_mx(
                 out=g_codes[:, i, :].bitcast(FP8X4),
                 scales=g_planes[:, i, :],
-                in_=grouped_g[:].rearrange("p r j -> p (r j)"),
+                in_=grouped_g_of[i][:].rearrange("p r j -> p (r j)"),
             )
 
-        for i in range(TOKEN_TILES + LAG):
-            if i < TOKEN_TILES:
-                tanh_of_tile(i)
-            if i >= LAG:
-                quantise_g(i - LAG)
+        def first_stage_step(step):
+            if step < TOKEN_TILES:
+                add_of_tile(step)
+            if step < T:
+                turn_input(first_inputs + step)
+            if 1 <= step <= T:
+                quantise_input(first_inputs + step - 1)
+            if TURN_LAG <= step < TOKEN_TILES + TURN_LAG:
+                tanh_of_tile(step - TURN_LAG)
+            if QUANT_LAG <= step < TOKEN_TILES + QUANT_LAG:
+                quantise_g(step - QUANT_LAG)
+
+        z = {}
+        top = [soft.tile([P, H], F32, name="top%d" % c, tag="top") for c in range(B_TILES)]
+        top_b = [soft.tile([P, H], F32, name="top_b%d" % c, tag="top_b") for c in range(B_TILES)]
+        terms = [soft.tile([P, 2, T, H], F32, name="terms%d" % c, tag="terms") for c in range(B_TILES)]
+        totals = {}
+
+        def scores(c, t):
+            z_t = sums.tile([P, H], F32, tag="sums%d" % t)
+            nc.tensor.matmul_mx(
+                out=z_t[:],
+                lhsT=g_codes[:, c * T + t, :].bitcast(FP8X4),
+                lhsT_scale=g_planes[:, c * T + t, :],
+                rhs=w_a[:].bitcast(FP8X4),
+                rhs_scale=w_planes[PLANE_W_A:P, :],
+                start=True,
+                stop=True,
+            )
+            z[c, t] = z_t
+            if t == 0:
+                nc.scalar.copy(out=top[c][:], in_=z_t[:])
+            if t == 2:
+                nc.scalar.copy(out=top_b[c][:], in_=z_t[:])
+
+        def maximum(c):
+            nc.vector.tensor_max(out=top[c][:], in0=top[c][:], in1=z[c, 1][:])
+            nc.vector.tensor_max(out=top_b[c][:], in0=top_b[c][:], in1=z[c, 3][:])
+            nc.vector.tensor_max(out=top[c][:], in0=top[c][:], in1=z[c, 4][:])
+            nc.vector.tensor_max(out=top[c][:], in0=top[c][:], in1=top_b[c][:])
+
+        def shifted_exp(c, t):
+            nc.vector.tensor_sub(out=terms[c][:, 0, t, :], in0=z[c, t][:], in1=top[c][:])
+            nc.scalar.activation(out=terms[c][:, 0, t, :], in_=terms[c][:, 0, t, :], func=ACT.Exp)
+
+        def weigh(c, t):
+            nc.vector.tensor_mul(out=terms[c][:, 1, t, :], in0=terms[c][:, 0, t, :], in1=hi_sb[c][:, t, :])
+
+        def sum_over_t(c, kind):
+            total = turned.tile([P, H_SLICES, P], F32, tag="turned")
+            for s in range(H_SLICES):
+                for t in range(T):
+                    nc.tensor.matmul(
+                        out=total[:, s, :],
+                        lhsT=terms[c][:, kind, t, s * P : (s + 1) * P],
+                        rhs=ident_f32[:],
+                        is_transpose=True,
+                        start=(t == 0),
+                        stop=(t == T - 1),
+                    )
+            totals[c, kind] = total
+
+        def finish(c):
+            inverse = soft.tile([P, H_SLICES, P], F32)
+            nc.vector.reciprocal(out=inverse[:], in_=totals[c, 0][:])
+            pooled_t = soft.tile([P, H_SLICES, P], F32)
+            nc.vector.tensor_mul(out=pooled_t[:], in0=totals[c, 1][:], in1=inverse[:])
+            back = turned.tile([P, H_SLICES, P], F32, tag="turned")
+            for s in range(H_SLICES):
+                nc.tensor.transpose(back[:, s, :], pooled_t[:, s, :], ident_f32[:])
+            pooled = soft.tile([P, H], F32)
+            nc.scalar.copy(out=pooled[:], in_=back[:].rearrange("p s r -> p (s r)"))
+            nc.sync.dma_start(out=out[c * P : (c + 1) * P, :], in_=pooled[:])
+
+        for step in range(TOKEN_TILES):
+            first_stage_step(step)
+        for t in range(T):
+            scores(0, t)
+        maximum(0)
+        for step in range(TOKEN_TILES, TOKEN_TILES + QUANT_LAG):
+            first_stage_step(step)
 
         for c in range(B_TILES):
-            z = []
+            if c > 0:
+                maximum(c)
             for t in range(T):
-                z_t = sums.tile([P, H], F32, tag="sums%d" % t)
-                nc.tensor.matmul_mx(
-                    out=z_t[:],
-                    lhsT=g_codes[:, c * T + t, :].bitcast(FP8X4),
-                    lhsT_scale=g_planes[:, c * T + t, :],
-                    rhs=w_a[:].bitcast(FP8X4),
-                    rhs_scale=w_planes[PLANE_W_A:P, :],
-                    start=True,
-                    stop=True,
-                )
-                z.append(z_t)
-
-            top = soft.tile([P, H], F32)
-            top_b = soft.tile([P, H], F32)
-            nc.scalar.copy(out=top[:], in_=z[0][:])
-            nc.scalar.copy(out=top_b[:], in_=z[2][:])
-            nc.vector.tensor_max(out=top[:], in0=top[:], in1=z[1][:])
-            nc.vector.tensor_max(out=top_b[:], in0=top_b[:], in1=z[3][:])
-            nc.vector.tensor_max(out=top[:], in0=top[:], in1=z[4][:])
-            nc.vector.tensor_max(out=top[:], in0=top[:], in1=top_b[:])
-
-            terms = soft.tile([P, 2, T, H], F32)
+                shifted_exp(c, t)
+                if c + 1 < B_TILES:
+                    scores(c + 1, t)
+            if c > 0:
+                finish(c - 1)
             for t in range(T):
-                nc.vector.tensor_sub(out=terms[:, 0, t, :], in0=z[t][:], in1=top[:])
-                nc.scalar.activation(out=terms[:, 0, t, :], in_=terms[:, 0, t, :], func=ACT.Exp)
-            for t in range(T):
-                nc.vector.tensor_mul(out=terms[:, 1, t, :], in0=terms[:, 0, t, :], in1=hi_sb[c][:, t, :])
-
-            nc.vector.tensor_add(out=terms[:, :, 0:2, :], in0=terms[:, :, 0:2, :], in1=terms[:, :, 2:4, :])
-            nc.vector.tensor_add(out=terms[:, :, 0, :], in0=terms[:, :, 0, :], in1=terms[:, :, 1, :])
-            nc.vector.tensor_add(out=terms[:, :, 0, :], in0=terms[:, :, 0, :], in1=terms[:, :, 4, :])
-
-            inverse = soft.tile([P, H], F32)
-            nc.vector.reciprocal(out=inverse[:], in_=terms[:, 0, 0, :])
-            pooled = soft.tile([P, H], F32)
-            nc.vector.tensor_mul(out=pooled[:], in0=terms[:, 1, 0, :], in1=inverse[:])
-            nc.sync.dma_start(out=out[c * P : (c + 1) * P, :], in_=pooled[:])
+                weigh(c, t)
+            sum_over_t(c, 0)
+            sum_over_t(c, 1)
+        finish(B_TILES - 1)

@@ -64,6 +64,7 @@ def tile_haint_attention_kernel(
 ):
     nc = tc.nc
     with ExitStack() as ctx:
+        ctx.enter_context(tc.manual_schedule())
         keep = ctx.enter_context(tc.tile_pool(name="keep", bufs=1))
         stage = ctx.enter_context(tc.tile_pool(name="stage", bufs=3))
         soft = ctx.enter_context(tc.tile_pool(name="soft", bufs=B_TILES))

@@ -17,11 +17,14 @@ B, T, H, A = 256, 5, 512, 512
 B_TILES = B // P
 TOKEN_TILES = B_TILES * T
 H_SLICES = H // P
-Q_INPUTS = 2 * B_TILES
-INPUTS = Q_INPUTS + TOKEN_TILES
+TILE_INPUTS = 2 + T
+INPUTS = B_TILES * TILE_INPUTS
 
 TURN_LAG = 1
 QUANT_LAG = 3
+STATE_STEP = 3
+SCORE_LAG = 7
+STEPS = SCORE_LAG + T + 1
 
 PLANE_W_AS = (0, 4)
 PLANE_W_AH = 8
@@ -66,7 +69,7 @@ def tile_haint_attention_kernel(
     with ExitStack() as ctx:
         ctx.enter_context(tc.manual_schedule())
         keep = ctx.enter_context(tc.tile_pool(name="keep", bufs=1))
-        stage = ctx.enter_context(tc.tile_pool(name="stage", bufs=3))
+        stage = ctx.enter_context(tc.tile_pool(name="stage", bufs=4))
         soft = ctx.enter_context(tc.tile_pool(name="soft", bufs=B_TILES))
         turned = ctx.enter_context(tc.psum_pool(name="turned", bufs=3))
         sums = ctx.enter_context(tc.psum_pool(name="sums", bufs=1))
@@ -101,17 +104,19 @@ def tile_haint_attention_kernel(
         x_planes = keep.tile([P, INPUTS, P], U8, align_bytes=64)
         g_codes = keep.tile([P, TOKEN_TILES, P], U32, align_bytes=64)
         g_planes = keep.tile([P, TOKEN_TILES, P], U8, align_bytes=64)
-        sources = [(ht_sb, ct_sb)[half][:, c, :] for c in range(B_TILES) for half in range(2)]
-        sources.extend([hi_sb[c][:, t, :] for c in range(B_TILES) for t in range(T)])
+        sources = []
+        for c in range(B_TILES):
+            sources.extend([ht_sb[:, c, :], ct_sb[:, c, :]])
+            sources.extend([hi_sb[c][:, t, :] for t in range(T)])
         grouped_inputs = {}
 
         def turn_input(k):
-            words_t = turned.tile([P, 2, P], F32, tag="turned")
+            words_t = sums.tile([P, 2, P], F32, tag="sums%d" % (k % 3))
             words = sources[k].bitcast(F32)
             for u in range(2):
                 nc.tensor.transpose(words_t[:, u, :], words[:, u : H // 2 : 2], ident_f32[:])
             grouped = stage.tile([P, P, PACK], BF16, align_bytes=64)
-            copy_out = nc.vector.tensor_copy if k < Q_INPUTS else nc.scalar.copy
+            copy_out = nc.vector.tensor_copy if (k < TILE_INPUTS and k % 2 == 0) else nc.scalar.copy
             copy_out(out=grouped[:].bitcast(F32), in_=words_t[:].rearrange("p u r -> p r u"))
             grouped_inputs[k] = grouped
 
@@ -122,29 +127,28 @@ def tile_haint_attention_kernel(
                 in_=grouped_inputs[k][:].rearrange("p r j -> p (r j)"),
             )
 
-        first_inputs = Q_INPUTS + T
-        for k in range(first_inputs + 1):
-            if k < first_inputs:
-                turn_input(k)
-            if k > 0:
-                quantise_input(k - 1)
-
         as_ba = [keep.tile([P, PACK, P], F32, name="as_ba%d" % c) for c in range(B_TILES)]
-        for c in range(B_TILES):
-            a_s = sums.tile([P, A], F32, tag="sums%d" % (3 + c))
+
+        a_s_of = {}
+
+        def state(c):
+            a_s = turned.tile([P, A], F32, tag="turned")
             for half in range(2):
                 nc.tensor.matmul_mx(
                     out=a_s[:],
-                    lhsT=x_codes[:, 2 * c + half, :].bitcast(FP8X4),
-                    lhsT_scale=x_planes[:, 2 * c + half, :],
+                    lhsT=x_codes[:, TILE_INPUTS * c + half, :].bitcast(FP8X4),
+                    lhsT_scale=x_planes[:, TILE_INPUTS * c + half, :],
                     rhs=w_as[:, half, :].bitcast(FP8X4),
                     rhs_scale=w_planes[PLANE_W_AS[half] : P, :],
                     start=(half == 0),
                     stop=(half == 1),
                 )
+            a_s_of[c] = a_s
+
+        def add_bias(c):
             nc.vector.tensor_add(
                 out=as_ba[c][:],
-                in0=a_s[:].rearrange("p (r j) -> p j r", j=PACK),
+                in0=a_s_of[c][:].rearrange("p (r j) -> p j r", j=PACK),
                 in1=ba_all[:].rearrange("p (r j) -> p j r", j=PACK),
             )
 
@@ -152,25 +156,26 @@ def tile_haint_attention_kernel(
         grouped_g_of = {}
 
         def add_of_tile(i):
+            c, t = divmod(i, T)
             ah = sums.tile([P, A], F32, tag="sums%d" % (3 + i % 2))
             nc.tensor.matmul_mx(
                 out=ah[:],
-                lhsT=x_codes[:, Q_INPUTS + i, :].bitcast(FP8X4),
-                lhsT_scale=x_planes[:, Q_INPUTS + i, :],
+                lhsT=x_codes[:, TILE_INPUTS * c + 2 + t, :].bitcast(FP8X4),
+                lhsT_scale=x_planes[:, TILE_INPUTS * c + 2 + t, :],
                 rhs=w_ah[:].bitcast(FP8X4),
                 rhs_scale=w_planes[PLANE_W_AH:P, :],
                 start=True,
                 stop=True,
             )
             pre = stage.tile([P, PACK, P], F32)
-            nc.vector.tensor_add(out=pre[:], in0=ah[:].rearrange("p (r j) -> p j r", j=PACK), in1=as_ba[i // T][:])
+            nc.vector.tensor_add(out=pre[:], in0=ah[:].rearrange("p (r j) -> p j r", j=PACK), in1=as_ba[c][:])
             pre_of[i] = pre
 
         def tanh_of_tile(i):
             pre_t = turned.tile([P, PACK, P], F32, tag="turned")
             for j in range(PACK):
                 nc.tensor.transpose(pre_t[:, j, :], pre_of[i][:, j, :], ident_f32[:])
-            grouped_g = stage.tile([P, P, PACK], BF16, align_bytes=64, bufs=QUANT_LAG + 1)
+            grouped_g = stage.tile([P, P, PACK], BF16, align_bytes=64, bufs=QUANT_LAG + 2)
             nc.scalar.activation(out=grouped_g[:], in_=pre_t[:].rearrange("p j r -> p r j"), func=ACT.Tanh)
             grouped_g_of[i] = grouped_g
 
@@ -181,23 +186,10 @@ def tile_haint_attention_kernel(
                 in_=grouped_g_of[i][:].rearrange("p r j -> p (r j)"),
             )
 
-        def first_stage_step(step):
-            if step < TOKEN_TILES:
-                add_of_tile(step)
-            if step < T:
-                turn_input(first_inputs + step)
-            if 1 <= step <= T:
-                quantise_input(first_inputs + step - 1)
-            if TURN_LAG <= step < TOKEN_TILES + TURN_LAG:
-                tanh_of_tile(step - TURN_LAG)
-            if QUANT_LAG <= step < TOKEN_TILES + QUANT_LAG:
-                quantise_g(step - QUANT_LAG)
-
         z = {}
         top = [soft.tile([P, H], F32, name="top%d" % c, tag="top") for c in range(B_TILES)]
-        top_b = [soft.tile([P, H], F32, name="top_b%d" % c, tag="top_b") for c in range(B_TILES)]
         terms = [soft.tile([P, 2, T, H], F32, name="terms%d" % c, tag="terms") for c in range(B_TILES)]
-        totals = {}
+        inverse = [soft.tile([P, H_SLICES, P], F32, name="inverse%d" % c, tag="inverse") for c in range(B_TILES)]
 
         def scores(c, t):
             z_t = sums.tile([P, H], F32, tag="sums%d" % t)
@@ -213,67 +205,108 @@ def tile_haint_attention_kernel(
             z[c, t] = z_t
             if t == 0:
                 nc.scalar.copy(out=top[c][:], in_=z_t[:])
-            if t == 2:
-                nc.scalar.copy(out=top_b[c][:], in_=z_t[:])
 
-        def maximum(c):
-            nc.vector.tensor_max(out=top[c][:], in0=top[c][:], in1=z[c, 1][:])
-            nc.vector.tensor_max(out=top_b[c][:], in0=top_b[c][:], in1=z[c, 3][:])
-            nc.vector.tensor_max(out=top[c][:], in0=top[c][:], in1=z[c, 4][:])
-            nc.vector.tensor_max(out=top[c][:], in0=top[c][:], in1=top_b[c][:])
+        def raise_maximum(c, t):
+            nc.vector.tensor_max(out=top[c][:], in0=top[c][:], in1=z[c, t][:])
 
         def shifted_exp(c, t):
             nc.vector.tensor_sub(out=terms[c][:, 0, t, :], in0=z[c, t][:], in1=top[c][:])
             nc.scalar.activation(out=terms[c][:, 0, t, :], in_=terms[c][:, 0, t, :], func=ACT.Exp)
 
-        def weigh(c, t):
-            nc.vector.tensor_mul(out=terms[c][:, 1, t, :], in0=terms[c][:, 0, t, :], in1=hi_sb[c][:, t, :])
+        def weigh_step(c, t):
+            nc.gpsimd.tensor_mul(out=terms[c][:, 1, t, :], in0=terms[c][:, 0, t, :], in1=hi_sb[c][:, t, :])
 
-        def sum_over_t(c, kind):
-            total = turned.tile([P, H_SLICES, P], F32, tag="turned")
-            for s in range(H_SLICES):
+        def weigh_slices(c, slices):
+            cols = slice(slices[0] * P, (slices[-1] + 1) * P)
+            nc.vector.tensor_mul(out=terms[c][:, 1, :, cols], in0=terms[c][:, 0, :, cols], in1=hi_sb[c][:, :, cols])
+
+        def sum_over_t(total, c, kind, slices):
+            for n, s in enumerate(slices):
                 for t in range(T):
                     nc.tensor.matmul(
-                        out=total[:, s, :],
+                        out=total[:, n, :],
                         lhsT=terms[c][:, kind, t, s * P : (s + 1) * P],
                         rhs=ident_f32[:],
                         is_transpose=True,
                         start=(t == 0),
                         stop=(t == T - 1),
                     )
-            totals[c, kind] = total
 
-        def finish(c):
-            inverse = soft.tile([P, H_SLICES, P], F32)
-            nc.vector.reciprocal(out=inverse[:], in_=totals[c, 0][:])
-            pooled_t = soft.tile([P, H_SLICES, P], F32)
-            nc.vector.tensor_mul(out=pooled_t[:], in0=totals[c, 1][:], in1=inverse[:])
-            back = turned.tile([P, H_SLICES, P], F32, tag="turned")
-            for s in range(H_SLICES):
-                nc.tensor.transpose(back[:, s, :], pooled_t[:, s, :], ident_f32[:])
-            pooled = soft.tile([P, H], F32)
+        def invert(c, e_total):
+            nc.vector.reciprocal(out=inverse[c][:], in_=e_total[:])
+
+        def divide_and_store(c, weighted_total, back, slices):
+            n_slices = len(slices)
+            pooled_t = soft.tile([P, n_slices, P], F32, tag="pooled_t%d" % n_slices)
+            nc.vector.tensor_mul(
+                out=pooled_t[:], in0=weighted_total[:], in1=inverse[c][:, slices[0] : slices[-1] + 1, :]
+            )
+            for n in range(n_slices):
+                nc.tensor.transpose(back[:, n, :], pooled_t[:, n, :], ident_f32[:])
+            pooled = soft.tile([P, n_slices * P], F32, tag="pooled%d" % n_slices)
             nc.scalar.copy(out=pooled[:], in_=back[:].rearrange("p s r -> p (s r)"))
-            nc.sync.dma_start(out=out[c * P : (c + 1) * P, :], in_=pooled[:])
+            nc.sync.dma_start(
+                out=out[c * P : (c + 1) * P, slices[0] * P : (slices[-1] + 1) * P], in_=pooled[:]
+            )
 
-        for step in range(TOKEN_TILES):
-            first_stage_step(step)
+        for k in range(TILE_INPUTS + 1):
+            if k < TILE_INPUTS:
+                turn_input(k)
+            if k > 0:
+                quantise_input(k - 1)
+        state(0)
+        add_bias(0)
+
+        for step in range(STEPS):
+            if step == STATE_STEP + 1:
+                add_bias(1)
+            if step < TOKEN_TILES:
+                add_of_tile(step)
+            if step == STATE_STEP:
+                state(1)
+            if step < TILE_INPUTS:
+                turn_input(TILE_INPUTS + step)
+            if 1 <= step <= TILE_INPUTS:
+                quantise_input(TILE_INPUTS + step - 1)
+            if TURN_LAG <= step < TOKEN_TILES + TURN_LAG:
+                tanh_of_tile(step - TURN_LAG)
+            if QUANT_LAG <= step < TOKEN_TILES + QUANT_LAG:
+                quantise_g(step - QUANT_LAG)
+            if SCORE_LAG <= step < SCORE_LAG + T:
+                scores(0, step - SCORE_LAG)
+            if SCORE_LAG + 1 < step:
+                raise_maximum(0, step - SCORE_LAG - 1)
+
+        all_slices = (0, 1, 2, 3)
+        halves = ((0, 1), (2, 3))
+
         for t in range(T):
-            scores(0, t)
-        maximum(0)
-        for step in range(TOKEN_TILES, TOKEN_TILES + QUANT_LAG):
-            first_stage_step(step)
+            shifted_exp(0, t)
+            weigh_step(0, t)
+            scores(1, t)
+            if t > 1:
+                raise_maximum(1, t - 1)
+        raise_maximum(1, T - 1)
+        e_total_0 = turned.tile([P, H_SLICES, P], F32, tag="turned")
+        weighted_total_0 = turned.tile([P, H_SLICES, P], F32, tag="turned")
+        back_0 = turned.tile([P, H_SLICES, P], F32, tag="turned")
+        sum_over_t(e_total_0, 0, 0, all_slices)
+        sum_over_t(weighted_total_0, 0, 1, all_slices)
 
-        for c in range(B_TILES):
-            if c > 0:
-                maximum(c)
-            for t in range(T):
-                shifted_exp(c, t)
-                if c + 1 < B_TILES:
-                    scores(c + 1, t)
-            if c > 0:
-                finish(c - 1)
-            for t in range(T):
-                weigh(c, t)
-            sum_over_t(c, 0)
-            sum_over_t(c, 1)
-        finish(B_TILES - 1)
+        for t in range(T):
+            shifted_exp(1, t)
+        e_total_1 = sums.tile([P, H_SLICES, P], F32, tag="sums4")
+        sum_over_t(e_total_1, 1, 0, all_slices)
+        invert(0, e_total_0)
+        weighted_totals_1 = []
+        for n, slices in enumerate(halves):
+            weigh_slices(1, slices)
+            weighted_total = sums.tile([P, 2, P], F32, tag="sums%d" % n)
+            sum_over_t(weighted_total, 1, 1, slices)
+            weighted_totals_1.append(weighted_total)
+            if n == 0:
+                divide_and_store(0, weighted_total_0, back_0, all_slices)
+        invert(1, e_total_1)
+        for n, slices in enumerate(halves):
+            back = sums.tile([P, 2, P], F32, tag="sums%d" % (2 + n))
+            divide_and_store(1, weighted_totals_1[n], back, slices)

@@ -17,14 +17,16 @@ B, T, H, A = 256, 5, 512, 512
 B_TILES = B // P
 TOKEN_TILES = B_TILES * T
 H_SLICES = H // P
-TILE_INPUTS = 2 + T
-INPUTS = B_TILES * TILE_INPUTS
+Q_INPUTS = 2 * B_TILES
+INPUTS = Q_INPUTS + TOKEN_TILES
+EARLY_INPUTS = Q_INPUTS + T
 
 TURN_LAG = 1
 QUANT_LAG = 3
-STATE_STEP = 3
-SCORE_LAG = 7
-STEPS = SCORE_LAG + T + 1
+STEPS = TOKEN_TILES + QUANT_LAG
+STATE_STEP = 2
+INPUT_STEP = 2
+SCORE_LAG = 6
 
 PLANE_W_AS = (0, 4)
 PLANE_W_AH = 8
@@ -70,7 +72,6 @@ def tile_haint_attention_kernel(
         ctx.enter_context(tc.manual_schedule())
         keep = ctx.enter_context(tc.tile_pool(name="keep", bufs=1))
         stage = ctx.enter_context(tc.tile_pool(name="stage", bufs=4))
-        soft = ctx.enter_context(tc.tile_pool(name="soft", bufs=B_TILES))
         turned = ctx.enter_context(tc.psum_pool(name="turned", bufs=3))
         sums = ctx.enter_context(tc.psum_pool(name="sums", bufs=1))
 
@@ -78,11 +79,16 @@ def tile_haint_attention_kernel(
         nc.vector.memset(w_planes[:].bitcast(I32), 0)
         ident_f32 = keep.tile([P, P], F32)
         make_identity(nc, ident_f32[:])
+        ba_row = keep.tile([P, A], BF16)
+        nc.vector.memset(ba_row[:], 0.0)
+        ones = keep.tile([P, P], BF16)
+        nc.vector.memset(ones[:], 1.0)
 
         ht_sb = keep.tile([P, B_TILES, H], BF16)
         ct_sb = keep.tile([P, B_TILES, H], BF16)
         nc.sync.dma_start(out=ht_sb[:], in_=ht.rearrange("(c p) k -> p c k", p=P))
         nc.sync.dma_start(out=ct_sb[:], in_=ct.rearrange("(c p) k -> p c k", p=P))
+        nc.sync.dma_start(out=ba_row[0:1, :], in_=ba)
         hi_sb = [keep.tile([P, T, H], BF16, name="hi_sb%d" % c) for c in range(B_TILES)]
         nc.sync.dma_start(out=hi_sb[0][:], in_=hi[0:P])
 
@@ -94,8 +100,6 @@ def tile_haint_attention_kernel(
         load_words(nc, w_as[:, 0, :], W_as_words[0])
         load_words(nc, w_as[:, 1, :], W_as_words[1])
         load_words(nc, w_ah[:], W_ah_words[0])
-        ba_all = keep.tile([P, A], BF16)
-        nc.sync.dma_start(out=ba_all[:], in_=ba.rearrange("o a -> (o a)").partition_broadcast(P))
         nc.sync.dma_start(out=hi_sb[1][:], in_=hi[P : 2 * P])
         load_scale_rows(nc, w_planes, PLANE_W_A, W_a_scales)
         load_words(nc, w_a[:], W_a_words[0])
@@ -104,10 +108,8 @@ def tile_haint_attention_kernel(
         x_planes = keep.tile([P, INPUTS, P], U8, align_bytes=64)
         g_codes = keep.tile([P, TOKEN_TILES, P], U32, align_bytes=64)
         g_planes = keep.tile([P, TOKEN_TILES, P], U8, align_bytes=64)
-        sources = []
-        for c in range(B_TILES):
-            sources.extend([ht_sb[:, c, :], ct_sb[:, c, :]])
-            sources.extend([hi_sb[c][:, t, :] for t in range(T)])
+        sources = [(ht_sb, ct_sb)[half][:, c, :] for c in range(B_TILES) for half in range(2)]
+        sources.extend([hi_sb[c][:, t, :] for c in range(B_TILES) for t in range(T)])
         grouped_inputs = {}
 
         def turn_input(k):
@@ -116,7 +118,7 @@ def tile_haint_attention_kernel(
             for u in range(2):
                 nc.tensor.transpose(words_t[:, u, :], words[:, u : H // 2 : 2], ident_f32[:])
             grouped = stage.tile([P, P, PACK], BF16, align_bytes=64)
-            copy_out = nc.vector.tensor_copy if (k < TILE_INPUTS and k % 2 == 0) else nc.scalar.copy
+            copy_out = nc.vector.tensor_copy if (k < EARLY_INPUTS and k % 2 == 0) else nc.scalar.copy
             copy_out(out=grouped[:].bitcast(F32), in_=words_t[:].rearrange("p u r -> p r u"))
             grouped_inputs[k] = grouped
 
@@ -128,16 +130,21 @@ def tile_haint_attention_kernel(
             )
 
         as_ba = [keep.tile([P, PACK, P], F32, name="as_ba%d" % c) for c in range(B_TILES)]
-
         a_s_of = {}
+        ba_all = keep.tile([P, PACK, P], F32)
+
+        def spread_bias():
+            ba_sum = turned.tile([P, A], F32, tag="turned")
+            nc.tensor.matmul(out=ba_sum[:], lhsT=ones[:], rhs=ba_row[:], start=True, stop=True)
+            nc.scalar.copy(out=ba_all[:], in_=ba_sum[:].rearrange("p (r j) -> p j r", j=PACK))
 
         def state(c):
             a_s = turned.tile([P, A], F32, tag="turned")
             for half in range(2):
                 nc.tensor.matmul_mx(
                     out=a_s[:],
-                    lhsT=x_codes[:, TILE_INPUTS * c + half, :].bitcast(FP8X4),
-                    lhsT_scale=x_planes[:, TILE_INPUTS * c + half, :],
+                    lhsT=x_codes[:, 2 * c + half, :].bitcast(FP8X4),
+                    lhsT_scale=x_planes[:, 2 * c + half, :],
                     rhs=w_as[:, half, :].bitcast(FP8X4),
                     rhs_scale=w_planes[PLANE_W_AS[half] : P, :],
                     start=(half == 0),
@@ -149,26 +156,25 @@ def tile_haint_attention_kernel(
             nc.vector.tensor_add(
                 out=as_ba[c][:],
                 in0=a_s_of[c][:].rearrange("p (r j) -> p j r", j=PACK),
-                in1=ba_all[:].rearrange("p (r j) -> p j r", j=PACK),
+                in1=ba_all[:],
             )
 
         pre_of = {}
         grouped_g_of = {}
 
         def add_of_tile(i):
-            c, t = divmod(i, T)
             ah = sums.tile([P, A], F32, tag="sums%d" % (3 + i % 2))
             nc.tensor.matmul_mx(
                 out=ah[:],
-                lhsT=x_codes[:, TILE_INPUTS * c + 2 + t, :].bitcast(FP8X4),
-                lhsT_scale=x_planes[:, TILE_INPUTS * c + 2 + t, :],
+                lhsT=x_codes[:, Q_INPUTS + i, :].bitcast(FP8X4),
+                lhsT_scale=x_planes[:, Q_INPUTS + i, :],
                 rhs=w_ah[:].bitcast(FP8X4),
                 rhs_scale=w_planes[PLANE_W_AH:P, :],
                 start=True,
                 stop=True,
             )
             pre = stage.tile([P, PACK, P], F32)
-            nc.vector.tensor_add(out=pre[:], in0=ah[:].rearrange("p (r j) -> p j r", j=PACK), in1=as_ba[c][:])
+            nc.vector.tensor_add(out=pre[:], in0=ah[:].rearrange("p (r j) -> p j r", j=PACK), in1=as_ba[i // T][:])
             pre_of[i] = pre
 
         def tanh_of_tile(i):
@@ -187,9 +193,8 @@ def tile_haint_attention_kernel(
             )
 
         z = {}
-        top = [soft.tile([P, H], F32, name="top%d" % c, tag="top") for c in range(B_TILES)]
-        terms = [soft.tile([P, 2, T, H], F32, name="terms%d" % c, tag="terms") for c in range(B_TILES)]
-        inverse = [soft.tile([P, H_SLICES, P], F32, name="inverse%d" % c, tag="inverse") for c in range(B_TILES)]
+        top = [keep.tile([P, H], F32, name="top%d" % c) for c in range(B_TILES)]
+        terms = [keep.tile([P, 2, T, H], F32, name="terms%d" % c) for c in range(B_TILES)]
 
         def scores(c, t):
             z_t = sums.tile([P, H], F32, tag="sums%d" % t)
@@ -213,12 +218,7 @@ def tile_haint_attention_kernel(
             nc.vector.tensor_sub(out=terms[c][:, 0, t, :], in0=z[c, t][:], in1=top[c][:])
             nc.scalar.activation(out=terms[c][:, 0, t, :], in_=terms[c][:, 0, t, :], func=ACT.Exp)
 
-        def weigh_step(c, t):
-            nc.gpsimd.tensor_mul(out=terms[c][:, 1, t, :], in0=terms[c][:, 0, t, :], in1=hi_sb[c][:, t, :])
-
-        def weigh_slices(c, slices):
-            cols = slice(slices[0] * P, (slices[-1] + 1) * P)
-            nc.vector.tensor_mul(out=terms[c][:, 1, :, cols], in0=terms[c][:, 0, :, cols], in1=hi_sb[c][:, :, cols])
+        inverse = [keep.tile([P, H_SLICES, P], F32, name="inverse%d" % c) for c in range(B_TILES)]
 
         def sum_over_t(total, c, kind, slices):
             for n, s in enumerate(slices):
@@ -232,28 +232,27 @@ def tile_haint_attention_kernel(
                         stop=(t == T - 1),
                     )
 
-        def invert(c, e_total):
-            nc.vector.reciprocal(out=inverse[c][:], in_=e_total[:])
-
         def divide_and_store(c, weighted_total, back, slices):
             n_slices = len(slices)
-            pooled_t = soft.tile([P, n_slices, P], F32, tag="pooled_t%d" % n_slices)
+            pooled_t = stage.tile([P, n_slices, P], F32, tag="pooled_t", bufs=2)
             nc.vector.tensor_mul(
                 out=pooled_t[:], in0=weighted_total[:], in1=inverse[c][:, slices[0] : slices[-1] + 1, :]
             )
             for n in range(n_slices):
                 nc.tensor.transpose(back[:, n, :], pooled_t[:, n, :], ident_f32[:])
-            pooled = soft.tile([P, n_slices * P], F32, tag="pooled%d" % n_slices)
+            pooled = stage.tile([P, n_slices * P], F32, tag="pooled", bufs=2)
             nc.scalar.copy(out=pooled[:], in_=back[:].rearrange("p s r -> p (s r)"))
             nc.sync.dma_start(
                 out=out[c * P : (c + 1) * P, slices[0] * P : (slices[-1] + 1) * P], in_=pooled[:]
             )
 
-        for k in range(TILE_INPUTS + 1):
-            if k < TILE_INPUTS:
+        for k in range(EARLY_INPUTS + 1):
+            if k < EARLY_INPUTS:
                 turn_input(k)
             if k > 0:
                 quantise_input(k - 1)
+            if k == Q_INPUTS - 1:
+                spread_bias()
         state(0)
         add_bias(0)
 
@@ -264,17 +263,17 @@ def tile_haint_attention_kernel(
                 add_of_tile(step)
             if step == STATE_STEP:
                 state(1)
-            if step < TILE_INPUTS:
-                turn_input(TILE_INPUTS + step)
-            if 1 <= step <= TILE_INPUTS:
-                quantise_input(TILE_INPUTS + step - 1)
+            if INPUT_STEP <= step < INPUT_STEP + T:
+                turn_input(EARLY_INPUTS + step - INPUT_STEP)
+            if INPUT_STEP < step <= INPUT_STEP + T:
+                quantise_input(EARLY_INPUTS + step - INPUT_STEP - 1)
             if TURN_LAG <= step < TOKEN_TILES + TURN_LAG:
                 tanh_of_tile(step - TURN_LAG)
-            if QUANT_LAG <= step < TOKEN_TILES + QUANT_LAG:
+            if QUANT_LAG <= step:
                 quantise_g(step - QUANT_LAG)
             if SCORE_LAG <= step < SCORE_LAG + T:
                 scores(0, step - SCORE_LAG)
-            if SCORE_LAG + 1 < step:
+            if SCORE_LAG + 1 < step <= SCORE_LAG + T:
                 raise_maximum(0, step - SCORE_LAG - 1)
 
         all_slices = (0, 1, 2, 3)
@@ -282,7 +281,7 @@ def tile_haint_attention_kernel(
 
         for t in range(T):
             shifted_exp(0, t)
-            weigh_step(0, t)
+            nc.gpsimd.tensor_mul(out=terms[0][:, 1, t, :], in0=terms[0][:, 0, t, :], in1=hi_sb[0][:, t, :])
             scores(1, t)
             if t > 1:
                 raise_maximum(1, t - 1)
@@ -297,16 +296,17 @@ def tile_haint_attention_kernel(
             shifted_exp(1, t)
         e_total_1 = sums.tile([P, H_SLICES, P], F32, tag="sums4")
         sum_over_t(e_total_1, 1, 0, all_slices)
-        invert(0, e_total_0)
+        nc.vector.reciprocal(out=inverse[0][:], in_=e_total_0[:])
         weighted_totals_1 = []
         for n, slices in enumerate(halves):
-            weigh_slices(1, slices)
+            cols = slice(slices[0] * P, (slices[-1] + 1) * P)
+            nc.vector.tensor_mul(out=terms[1][:, 1, :, cols], in0=terms[1][:, 0, :, cols], in1=hi_sb[1][:, :, cols])
             weighted_total = sums.tile([P, 2, P], F32, tag="sums%d" % n)
             sum_over_t(weighted_total, 1, 1, slices)
             weighted_totals_1.append(weighted_total)
             if n == 0:
                 divide_and_store(0, weighted_total_0, back_0, all_slices)
-        invert(1, e_total_1)
+        nc.vector.reciprocal(out=inverse[1][:], in_=e_total_1[:])
         for n, slices in enumerate(halves):
             back = sums.tile([P, 2, P], F32, tag="sums%d" % (2 + n))
             divide_and_store(1, weighted_totals_1[n], back, slices)

@@ -69,7 +69,6 @@ def tile_haint_attention_kernel(
 ):
     nc = tc.nc
     with ExitStack() as ctx:
-        ctx.enter_context(tc.manual_schedule())
         keep = ctx.enter_context(tc.tile_pool(name="keep", bufs=1))
         stage = ctx.enter_context(tc.tile_pool(name="stage", bufs=4))
         turned = ctx.enter_context(tc.psum_pool(name="turned", bufs=3))

@@ -15,18 +15,7 @@ P = 128
 PACK = 4
 B, T, H, A = 256, 5, 512, 512
 B_TILES = B // P
-TOKEN_TILES = B_TILES * T
-H_SLICES = H // P
-Q_INPUTS = 2 * B_TILES
-INPUTS = Q_INPUTS + TOKEN_TILES
-EARLY_INPUTS = Q_INPUTS + T
-
-TURN_LAG = 1
-QUANT_LAG = 3
-STEPS = TOKEN_TILES + QUANT_LAG
-STATE_STEP = 2
-INPUT_STEP = 2
-SCORE_LAG = 6
+STEP_GROUPS = ((0, 2), (2, 4), (4, 5))
 
 PLANE_W_AS = (0, 4)
 PLANE_W_AH = 8
@@ -52,6 +41,12 @@ def load_words(nc, words_sb, words):
     )
 
 
+def regroup(nc, out, in_):
+    nc.vector.tensor_copy(
+        out=out.rearrange("p (j m) -> p j m", j=PACK), in_=in_.rearrange("p (m j) -> p j m", j=PACK)
+    )
+
+
 def tile_haint_attention_kernel(
     tc,
     ht,
@@ -70,142 +65,146 @@ def tile_haint_attention_kernel(
     nc = tc.nc
     with ExitStack() as ctx:
         keep = ctx.enter_context(tc.tile_pool(name="keep", bufs=1))
-        stage = ctx.enter_context(tc.tile_pool(name="stage", bufs=4))
-        turned = ctx.enter_context(tc.psum_pool(name="turned", bufs=3))
+        stage = ctx.enter_context(tc.tile_pool(name="stage", bufs=3))
+        pre_pool = ctx.enter_context(tc.psum_pool(name="pre_pool", bufs=3))
         sums = ctx.enter_context(tc.psum_pool(name="sums", bufs=1))
 
-        w_planes = keep.tile([P, A], U8, align_bytes=64)
-        nc.vector.memset(w_planes[:].bitcast(I32), 0)
+        warm = keep.tile([P, 1], F32)
+        nc.vector.memset(warm[:], 0.0)
+        nc.scalar.activation(out=warm[:], in_=warm[:], func=ACT.Tanh)
+        w_planes_raw = keep.tile([P, A], U8, align_bytes=64)
+        nc.vector.memset(w_planes_raw[:].bitcast(I32), 0)
         ident_f32 = keep.tile([P, P], F32)
         make_identity(nc, ident_f32[:])
-        ba_row = keep.tile([P, A], BF16)
-        nc.vector.memset(ba_row[:], 0.0)
-        ones = keep.tile([P, P], BF16)
-        nc.vector.memset(ones[:], 1.0)
 
-        ht_sb = keep.tile([P, B_TILES, H], BF16)
-        ct_sb = keep.tile([P, B_TILES, H], BF16)
-        nc.sync.dma_start(out=ht_sb[:], in_=ht.rearrange("(c p) k -> p c k", p=P))
-        nc.sync.dma_start(out=ct_sb[:], in_=ct.rearrange("(c p) k -> p c k", p=P))
-        nc.sync.dma_start(out=ba_row[0:1, :], in_=ba)
+        q_sb = [keep.tile([P, 2, H], BF16, name="q_sb%d" % c) for c in range(B_TILES)]
         hi_sb = [keep.tile([P, T, H], BF16, name="hi_sb%d" % c) for c in range(B_TILES)]
-        nc.sync.dma_start(out=hi_sb[0][:], in_=hi[0:P])
 
-        load_scale_rows(nc, w_planes, PLANE_W_AS[0], W_as_scales)
-        load_scale_rows(nc, w_planes, PLANE_W_AH, W_ah_scales)
-        w_as = keep.tile([P, 2, A], U32, align_bytes=64)
-        w_ah = keep.tile([P, A], U32, align_bytes=64)
-        w_a = keep.tile([P, H], U32, align_bytes=64)
-        load_words(nc, w_as[:, 0, :], W_as_words[0])
-        load_words(nc, w_as[:, 1, :], W_as_words[1])
-        load_words(nc, w_ah[:], W_ah_words[0])
-        nc.sync.dma_start(out=hi_sb[1][:], in_=hi[P : 2 * P])
-        load_scale_rows(nc, w_planes, PLANE_W_A, W_a_scales)
-        load_words(nc, w_a[:], W_a_words[0])
+        def load_batch_tile(c):
+            rows = slice(c * P, (c + 1) * P)
+            nc.sync.dma_start(out=q_sb[c][:, 0, :], in_=ht[rows])
+            nc.sync.dma_start(out=q_sb[c][:, 1, :], in_=ct[rows])
+            for t0, t1 in STEP_GROUPS:
+                nc.sync.dma_start(out=hi_sb[c][:, t0:t1, :], in_=hi[rows, t0:t1, :])
 
-        x_codes = keep.tile([P, INPUTS, P], U32, align_bytes=64)
-        x_planes = keep.tile([P, INPUTS, P], U8, align_bytes=64)
-        g_codes = keep.tile([P, TOKEN_TILES, P], U32, align_bytes=64)
-        g_planes = keep.tile([P, TOKEN_TILES, P], U8, align_bytes=64)
-        sources = [(ht_sb, ct_sb)[half][:, c, :] for c in range(B_TILES) for half in range(2)]
-        sources.extend([hi_sb[c][:, t, :] for c in range(B_TILES) for t in range(T)])
-        grouped_inputs = {}
+        load_batch_tile(0)
+        load_scale_rows(nc, w_planes_raw, PLANE_W_AS[0], W_as_scales)
+        load_scale_rows(nc, w_planes_raw, PLANE_W_AH, W_ah_scales)
+        load_scale_rows(nc, w_planes_raw, PLANE_W_A, W_a_scales)
+        w_raw = keep.tile([P, 4, A], U32, align_bytes=64)
+        w = keep.tile([P, 4, A], U32, align_bytes=64)
+        w_planes = keep.tile([P, A], U8, align_bytes=64)
+        load_words(nc, w_raw[:, 0, :], W_as_words[0])
+        load_words(nc, w_raw[:, 1, :], W_as_words[1])
+        load_words(nc, w_raw[:, 2, :], W_ah_words[0])
+        bias = keep.tile([P, PACK], BF16)
+        nc.sync.dma_start(out=bias[:], in_=ba.rearrange("o (p j) -> (o p) j", j=PACK))
+        load_batch_tile(1)
+        load_words(nc, w_raw[:, 3, :], W_a_words[0])
 
-        def turn_input(k):
-            words_t = sums.tile([P, 2, P], F32, tag="sums%d" % (k % 3))
-            words = sources[k].bitcast(F32)
-            for u in range(2):
-                nc.tensor.transpose(words_t[:, u, :], words[:, u : H // 2 : 2], ident_f32[:])
-            grouped = stage.tile([P, P, PACK], BF16, align_bytes=64)
-            copy_out = nc.vector.tensor_copy if (k < EARLY_INPUTS and k % 2 == 0) else nc.scalar.copy
-            copy_out(out=grouped[:].bitcast(F32), in_=words_t[:].rearrange("p u r -> p r u"))
-            grouped_inputs[k] = grouped
+        q_t = [keep.tile([P, 2, P, PACK], BF16, name="q_t%d" % c, align_bytes=64) for c in range(B_TILES)]
+        hi_t = [keep.tile([P, T, P, PACK], BF16, name="hi_t%d" % c, align_bytes=64) for c in range(B_TILES)]
+        q_codes = [keep.tile([P, 2, P], U32, name="q_codes%d" % c, align_bytes=64) for c in range(B_TILES)]
+        q_planes = [keep.tile([P, 2, P], U8, name="q_planes%d" % c, align_bytes=64) for c in range(B_TILES)]
+        hi_codes = [keep.tile([P, T, P], U32, name="hi_codes%d" % c, align_bytes=64) for c in range(B_TILES)]
+        hi_planes = [keep.tile([P, T, P], U8, name="hi_planes%d" % c, align_bytes=64) for c in range(B_TILES)]
+        g_codes = [keep.tile([P, T, P], U32, name="g_codes%d" % c, align_bytes=64) for c in range(B_TILES)]
+        g_planes = [keep.tile([P, T, P], U8, name="g_planes%d" % c, align_bytes=64) for c in range(B_TILES)]
 
-        def quantise_input(k):
+        turns = []
+
+        def turn(source, target, copy_out):
+            n = source.shape[1]
+            words_t = sums.tile([P, 2, 2, P], F32, tag="sums%d" % (2 + len(turns) % 3))
+            turns.append(n)
+            for i in range(n):
+                words = source[:, i, :].bitcast(F32)
+                for u in range(2):
+                    nc.tensor.transpose(words_t[:, i, u, :], words[:, u : H // 2 : 2], ident_f32[:])
+            copy_out(out=target.bitcast(F32), in_=words_t[:, 0:n].rearrange("p i u r -> p i r u"))
+
+        def quantise(codes, planes, grouped):
             nc.vector.quantize_mx(
-                out=x_codes[:, k, :].bitcast(FP8X4),
-                scales=x_planes[:, k, :],
-                in_=grouped_inputs[k][:].rearrange("p r j -> p (r j)"),
+                out=codes.rearrange("p i r -> p (i r)").bitcast(FP8X4),
+                scales=planes.rearrange("p i r -> p (i r)"),
+                in_=grouped.rearrange("p i r j -> p (i r j)"),
             )
 
-        as_ba = [keep.tile([P, PACK, P], F32, name="as_ba%d" % c) for c in range(B_TILES)]
-        a_s_of = {}
-        ba_all = keep.tile([P, PACK, P], F32)
+        def turn_q(c, copy_out):
+            turn(q_sb[c][:], q_t[c][:], copy_out)
 
-        def spread_bias():
-            ba_sum = turned.tile([P, A], F32, tag="turned")
-            nc.tensor.matmul(out=ba_sum[:], lhsT=ones[:], rhs=ba_row[:], start=True, stop=True)
-            nc.scalar.copy(out=ba_all[:], in_=ba_sum[:].rearrange("p (r j) -> p j r", j=PACK))
+        def quantise_q(c):
+            quantise(q_codes[c][:], q_planes[c][:], q_t[c][:])
 
-        def state(c):
-            a_s = turned.tile([P, A], F32, tag="turned")
-            for half in range(2):
-                nc.tensor.matmul_mx(
-                    out=a_s[:],
-                    lhsT=x_codes[:, 2 * c + half, :].bitcast(FP8X4),
-                    lhsT_scale=x_planes[:, 2 * c + half, :],
-                    rhs=w_as[:, half, :].bitcast(FP8X4),
-                    rhs_scale=w_planes[PLANE_W_AS[half] : P, :],
-                    start=(half == 0),
-                    stop=(half == 1),
-                )
-            a_s_of[c] = a_s
+        def turn_hi(c, s, copy_out):
+            t0, t1 = STEP_GROUPS[s]
+            turn(hi_sb[c][:, t0:t1, :], hi_t[c][:, t0:t1], copy_out)
 
-        def add_bias(c):
-            nc.vector.tensor_add(
-                out=as_ba[c][:],
-                in0=a_s_of[c][:].rearrange("p (r j) -> p j r", j=PACK),
-                in1=ba_all[:],
-            )
+        def quantise_hi(c, s):
+            t0, t1 = STEP_GROUPS[s]
+            quantise(hi_codes[c][:, t0:t1, :], hi_planes[c][:, t0:t1, :], hi_t[c][:, t0:t1])
 
-        pre_of = {}
-        grouped_g_of = {}
+        flat_g = {}
+        grouped_g = {}
 
-        def add_of_tile(i):
-            ah = sums.tile([P, A], F32, tag="sums%d" % (3 + i % 2))
-            nc.tensor.matmul_mx(
-                out=ah[:],
-                lhsT=x_codes[:, Q_INPUTS + i, :].bitcast(FP8X4),
-                lhsT_scale=x_planes[:, Q_INPUTS + i, :],
-                rhs=w_ah[:].bitcast(FP8X4),
-                rhs_scale=w_planes[PLANE_W_AH:P, :],
-                start=True,
-                stop=True,
-            )
-            pre = stage.tile([P, PACK, P], F32)
-            nc.vector.tensor_add(out=pre[:], in0=ah[:].rearrange("p (r j) -> p j r", j=PACK), in1=as_ba[i // T][:])
-            pre_of[i] = pre
+        def first_stage(c, s):
+            t0, t1 = STEP_GROUPS[s]
+            n = t1 - t0
+            blocks_per_bank = PACK // n
+            flat = stage.tile([P, PACK, n, P], BF16, tag="flat")
+            for j0 in range(0, PACK, blocks_per_bank):
+                pre = pre_pool.tile([P, blocks_per_bank, n, P], F32, tag="pre")
+                for j in range(j0, j0 + blocks_per_bank):
+                    cols = slice(j * P, (j + 1) * P)
+                    for t in range(t0, t1):
+                        moving = (
+                            (q_codes[c][:, 0, :], q_planes[c][:, 0, :], PLANE_W_AS[0]),
+                            (q_codes[c][:, 1, :], q_planes[c][:, 1, :], PLANE_W_AS[1]),
+                            (hi_codes[c][:, t, :], hi_planes[c][:, t, :], PLANE_W_AH),
+                        )
+                        for k, (codes, planes, first_row) in enumerate(moving):
+                            nc.tensor.matmul_mx(
+                                out=pre[:, j - j0, t - t0, :],
+                                lhsT=w[:, k, cols].bitcast(FP8X4),
+                                lhsT_scale=w_planes[first_row:P, cols],
+                                rhs=codes.bitcast(FP8X4),
+                                rhs_scale=planes,
+                                start=(k == 0),
+                                stop=(k == 2),
+                            )
+                for j in range(j0, j0 + blocks_per_bank):
+                    nc.scalar.activation(
+                        out=flat[:, j], in_=pre[:, j - j0], func=ACT.Tanh, bias=bias[:, j : j + 1]
+                    )
+            flat_g[c, s] = flat
 
-        def tanh_of_tile(i):
-            pre_t = turned.tile([P, PACK, P], F32, tag="turned")
-            for j in range(PACK):
-                nc.tensor.transpose(pre_t[:, j, :], pre_of[i][:, j, :], ident_f32[:])
-            grouped_g = stage.tile([P, P, PACK], BF16, align_bytes=64, bufs=QUANT_LAG + 2)
-            nc.scalar.activation(out=grouped_g[:], in_=pre_t[:].rearrange("p j r -> p r j"), func=ACT.Tanh)
-            grouped_g_of[i] = grouped_g
+        def group_g(c, s):
+            t0, t1 = STEP_GROUPS[s]
+            grouped = stage.tile([P, t1 - t0, P, PACK], BF16, tag="grouped", align_bytes=64)
+            nc.vector.tensor_copy(out=grouped[:], in_=flat_g[c, s][:].rearrange("p j i r -> p i r j"))
+            grouped_g[c, s] = grouped
 
-        def quantise_g(i):
-            nc.vector.quantize_mx(
-                out=g_codes[:, i, :].bitcast(FP8X4),
-                scales=g_planes[:, i, :],
-                in_=grouped_g_of[i][:].rearrange("p r j -> p (r j)"),
-            )
+        def quantise_g(c, s):
+            t0, t1 = STEP_GROUPS[s]
+            quantise(g_codes[c][:, t0:t1, :], g_planes[c][:, t0:t1, :], grouped_g[c, s][:])
 
         z = {}
-        top = [keep.tile([P, H], F32, name="top%d" % c) for c in range(B_TILES)]
-        terms = [keep.tile([P, 2, T, H], F32, name="terms%d" % c) for c in range(B_TILES)]
+        top = [keep.tile([P, PACK, P], F32, name="top%d" % c) for c in range(B_TILES)]
+        terms = [keep.tile([P, 2, T, PACK, P], F32, name="terms%d" % c) for c in range(B_TILES)]
 
         def scores(c, t):
-            z_t = sums.tile([P, H], F32, tag="sums%d" % t)
-            nc.tensor.matmul_mx(
-                out=z_t[:],
-                lhsT=g_codes[:, c * T + t, :].bitcast(FP8X4),
-                lhsT_scale=g_planes[:, c * T + t, :],
-                rhs=w_a[:].bitcast(FP8X4),
-                rhs_scale=w_planes[PLANE_W_A:P, :],
-                start=True,
-                stop=True,
-            )
+            z_t = sums.tile([P, PACK, P], F32, tag="sums%d" % t)
+            for j in range(PACK):
+                cols = slice(j * P, (j + 1) * P)
+                nc.tensor.matmul_mx(
+                    out=z_t[:, j, :],
+                    lhsT=w[:, 3, cols].bitcast(FP8X4),
+                    lhsT_scale=w_planes[PLANE_W_A:P, cols],
+                    rhs=g_codes[c][:, t, :].bitcast(FP8X4),
+                    rhs_scale=g_planes[c][:, t, :],
+                    start=True,
+                    stop=True,
+                )
             z[c, t] = z_t
             if t == 0:
                 nc.scalar.copy(out=top[c][:], in_=z_t[:])
@@ -214,98 +213,119 @@ def tile_haint_attention_kernel(
             nc.vector.tensor_max(out=top[c][:], in0=top[c][:], in1=z[c, t][:])
 
         def shifted_exp(c, t):
-            nc.vector.tensor_sub(out=terms[c][:, 0, t, :], in0=z[c, t][:], in1=top[c][:])
-            nc.scalar.activation(out=terms[c][:, 0, t, :], in_=terms[c][:, 0, t, :], func=ACT.Exp)
+            nc.vector.tensor_sub(out=terms[c][:, 0, t], in0=z[c, t][:], in1=top[c][:])
+            nc.scalar.activation(out=terms[c][:, 0, t], in_=terms[c][:, 0, t], func=ACT.Exp)
 
-        inverse = [keep.tile([P, H_SLICES, P], F32, name="inverse%d" % c) for c in range(B_TILES)]
+        def sum_over_t(total, c, kind, j):
+            for t in range(T):
+                nc.tensor.matmul(
+                    out=total[:, j, :],
+                    lhsT=terms[c][:, kind, t, j, :],
+                    rhs=ident_f32[:],
+                    is_transpose=True,
+                    start=(t == 0),
+                    stop=(t == T - 1),
+                )
 
-        def sum_over_t(total, c, kind, slices):
-            for n, s in enumerate(slices):
-                for t in range(T):
-                    nc.tensor.matmul(
-                        out=total[:, n, :],
-                        lhsT=terms[c][:, kind, t, s * P : (s + 1) * P],
-                        rhs=ident_f32[:],
-                        is_transpose=True,
-                        start=(t == 0),
-                        stop=(t == T - 1),
-                    )
-
-        def divide_and_store(c, weighted_total, back, slices):
-            n_slices = len(slices)
-            pooled_t = stage.tile([P, n_slices, P], F32, tag="pooled_t", bufs=2)
-            nc.vector.tensor_mul(
-                out=pooled_t[:], in0=weighted_total[:], in1=inverse[c][:, slices[0] : slices[-1] + 1, :]
+        def divide_and_store(c, e_total, weighted_total):
+            inverse = stage.tile([P, P, PACK], F32, tag="inverse", bufs=2)
+            nc.scalar.activation(
+                out=inverse[:], in_=e_total[:].rearrange("p j m -> p m j"), func=ACT.Abs_reciprocal_sqrt
             )
-            for n in range(n_slices):
-                nc.tensor.transpose(back[:, n, :], pooled_t[:, n, :], ident_f32[:])
-            pooled = stage.tile([P, n_slices * P], F32, tag="pooled", bufs=2)
-            nc.scalar.copy(out=pooled[:], in_=back[:].rearrange("p s r -> p (s r)"))
-            nc.sync.dma_start(
-                out=out[c * P : (c + 1) * P, slices[0] * P : (slices[-1] + 1) * P], in_=pooled[:]
+            nc.scalar.activation(out=inverse[:], in_=inverse[:], func=ACT.Square)
+            pooled = stage.tile([P, P, PACK], F32, tag="pooled", bufs=2)
+            nc.vector.tensor_mul(out=pooled[:], in0=weighted_total[:].rearrange("p j m -> p m j"), in1=inverse[:])
+            nc.sync.dma_start(out=out[c * P : (c + 1) * P, :], in_=pooled[:].rearrange("p m j -> p (m j)"))
+
+        vector_copy, scalar_copy = nc.vector.tensor_copy, nc.scalar.copy
+
+        turn_q(0, vector_copy)
+        turn_hi(0, 0, scalar_copy)
+        quantise_q(0)
+        turn_hi(0, 1, vector_copy)
+        quantise_hi(0, 0)
+        turn_hi(0, 2, scalar_copy)
+        quantise_hi(0, 1)
+        regroup(nc, w_planes[:], w_planes_raw[:])
+        quantise_hi(0, 2)
+        for k in range(3):
+            regroup(nc, w[:, k, :].bitcast(I32), w_raw[:, k, :].bitcast(I32))
+
+        first_stage(0, 0)
+        turn_q(1, scalar_copy)
+        first_stage(0, 1)
+        group_g(0, 0)
+        quantise_q(1)
+        turn_hi(1, 0, scalar_copy)
+        first_stage(0, 2)
+        group_g(0, 1)
+        quantise_g(0, 0)
+        turn_hi(1, 1, scalar_copy)
+        quantise_hi(1, 0)
+        regroup(nc, w[:, 3, :].bitcast(I32), w_raw[:, 3, :].bitcast(I32))
+        turn_hi(1, 2, scalar_copy)
+        group_g(0, 2)
+        quantise_g(0, 1)
+        quantise_hi(1, 1)
+        scores(0, 0)
+        scores(0, 1)
+        quantise_g(0, 2)
+        quantise_hi(1, 2)
+        first_stage(1, 0)
+        scores(0, 2)
+        scores(0, 3)
+        raise_maximum(0, 1)
+        raise_maximum(0, 2)
+        scores(0, 4)
+        raise_maximum(0, 3)
+        group_g(1, 0)
+        first_stage(1, 1)
+        raise_maximum(0, 4)
+        quantise_g(1, 0)
+        shifted_exp(0, 0)
+        first_stage(1, 2)
+        shifted_exp(0, 1)
+        group_g(1, 1)
+        scores(1, 0)
+        shifted_exp(0, 2)
+        quantise_g(1, 1)
+        scores(1, 1)
+        shifted_exp(0, 3)
+        group_g(1, 2)
+        scores(1, 2)
+        shifted_exp(0, 4)
+        quantise_g(1, 2)
+        scores(1, 3)
+        for t in range(T):
+            nc.gpsimd.tensor_mul(
+                out=terms[0][:, 1, t], in0=terms[0][:, 0, t], in1=hi_t[0][:, t].rearrange("p r j -> p j r")
             )
-
-        for k in range(EARLY_INPUTS + 1):
-            if k < EARLY_INPUTS:
-                turn_input(k)
-            if k > 0:
-                quantise_input(k - 1)
-            if k == Q_INPUTS - 1:
-                spread_bias()
-        state(0)
-        add_bias(0)
-
-        for step in range(STEPS):
-            if step == STATE_STEP + 1:
-                add_bias(1)
-            if step < TOKEN_TILES:
-                add_of_tile(step)
-            if step == STATE_STEP:
-                state(1)
-            if INPUT_STEP <= step < INPUT_STEP + T:
-                turn_input(EARLY_INPUTS + step - INPUT_STEP)
-            if INPUT_STEP < step <= INPUT_STEP + T:
-                quantise_input(EARLY_INPUTS + step - INPUT_STEP - 1)
-            if TURN_LAG <= step < TOKEN_TILES + TURN_LAG:
-                tanh_of_tile(step - TURN_LAG)
-            if QUANT_LAG <= step:
-                quantise_g(step - QUANT_LAG)
-            if SCORE_LAG <= step < SCORE_LAG + T:
-                scores(0, step - SCORE_LAG)
-            if SCORE_LAG + 1 < step <= SCORE_LAG + T:
-                raise_maximum(0, step - SCORE_LAG - 1)
-
-        all_slices = (0, 1, 2, 3)
-        halves = ((0, 1), (2, 3))
-
-        for t in range(T):
-            shifted_exp(0, t)
-            nc.gpsimd.tensor_mul(out=terms[0][:, 1, t, :], in0=terms[0][:, 0, t, :], in1=hi_sb[0][:, t, :])
-            scores(1, t)
-            if t > 1:
-                raise_maximum(1, t - 1)
-        raise_maximum(1, T - 1)
-        e_total_0 = turned.tile([P, H_SLICES, P], F32, tag="turned")
-        weighted_total_0 = turned.tile([P, H_SLICES, P], F32, tag="turned")
-        back_0 = turned.tile([P, H_SLICES, P], F32, tag="turned")
-        sum_over_t(e_total_0, 0, 0, all_slices)
-        sum_over_t(weighted_total_0, 0, 1, all_slices)
-
-        for t in range(T):
-            shifted_exp(1, t)
-        e_total_1 = sums.tile([P, H_SLICES, P], F32, tag="sums4")
-        sum_over_t(e_total_1, 1, 0, all_slices)
-        nc.vector.reciprocal(out=inverse[0][:], in_=e_total_0[:])
-        weighted_totals_1 = []
-        for n, slices in enumerate(halves):
-            cols = slice(slices[0] * P, (slices[-1] + 1) * P)
-            nc.vector.tensor_mul(out=terms[1][:, 1, :, cols], in0=terms[1][:, 0, :, cols], in1=hi_sb[1][:, :, cols])
-            weighted_total = sums.tile([P, 2, P], F32, tag="sums%d" % n)
-            sum_over_t(weighted_total, 1, 1, slices)
-            weighted_totals_1.append(weighted_total)
-            if n == 0:
-                divide_and_store(0, weighted_total_0, back_0, all_slices)
-        nc.vector.reciprocal(out=inverse[1][:], in_=e_total_1[:])
-        for n, slices in enumerate(halves):
-            back = sums.tile([P, 2, P], F32, tag="sums%d" % (2 + n))
-            divide_and_store(1, weighted_totals_1[n], back, slices)
+        raise_maximum(1, 1)
+        scores(1, 4)
+        for t in range(2, T):
+            raise_maximum(1, t)
+        with tc.manual_schedule(engines={mybir.EngineType.Activation}):
+            for t in range(T):
+                shifted_exp(1, t)
+            e_total_0 = pre_pool.tile([P, PACK, P], F32, tag="pre")
+            weighted_total_0 = pre_pool.tile([P, PACK, P], F32, tag="pre")
+            e_total_1 = pre_pool.tile([P, PACK, P], F32, tag="pre")
+            for j in range(PACK):
+                sum_over_t(e_total_0, 0, 0, j)
+            for j in range(PACK):
+                sum_over_t(weighted_total_0, 0, 1, j)
+            for j in range(PACK):
+                sum_over_t(e_total_1, 1, 0, j)
+            weighted_total_1 = sums.tile([P, PACK, P], F32, tag="sums0")
+            for j0 in range(0, PACK, 2):
+                js = slice(j0, j0 + 2)
+                nc.vector.tensor_mul(
+                    out=terms[1][:, 1, :, js],
+                    in0=terms[1][:, 0, :, js],
+                    in1=hi_t[1][:].rearrange("p t r j -> p t j r")[:, :, js],
+                )
+                for j in range(j0, j0 + 2):
+                    sum_over_t(weighted_total_1, 1, 1, j)
+                if j0 == 0:
+                    divide_and_store(0, e_total_0, weighted_total_0)
+            divide_and_store(1, e_total_1, weighted_total_1)

@@ -10,16 +10,17 @@ U32 = mybir.dt.uint32
 U8 = mybir.dt.uint8
 FP8X4 = mybir.dt.float8_e4m3fn_x4
 ACT = mybir.ActivationFunctionType
+ALU = mybir.AluOpType
 
 P = 128
 PACK = 4
 B, T, H, A = 256, 5, 512, 512
 B_TILES = B // P
-STEP_GROUPS = ((0, 2), (2, 4), (4, 5))
+STEP_GROUPS = (((0, 1), (1, 3), (3, 5)), ((0, 2), (2, 4), (4, 5)))
 
 PLANE_W_AS = (0, 4)
 PLANE_W_AH = 8
-PLANE_W_A = 12
+PLANE_W_A = 0
 
 FLOPS = 2 * B * (2 * H) * A + 2 * B * T * H * A + 2 * B * T * A * H
 
@@ -37,7 +38,7 @@ def load_scale_rows(nc, w_planes, first_row, scales):
 def load_words(nc, words_sb, words):
     nc.sync.dma_start(
         out=words_sb.bitcast(I32),
-        in_=words.rearrange("p n t -> p (n t)").bitcast(I32),
+        in_=words.rearrange("g p n t -> p g (n t)").bitcast(I32),
     )
 
 
@@ -72,35 +73,41 @@ def tile_haint_attention_kernel(
         warm = keep.tile([P, 1], F32)
         nc.vector.memset(warm[:], 0.0)
         nc.scalar.activation(out=warm[:], in_=warm[:], func=ACT.Tanh)
-        w_planes_raw = keep.tile([P, A], U8, align_bytes=64)
-        nc.vector.memset(w_planes_raw[:].bitcast(I32), 0)
+        g_scales_raw = keep.tile([P, A], U8, align_bytes=64)
+        z_scales_raw = keep.tile([P, A], U8, align_bytes=64)
+        nc.vector.memset(g_scales_raw[:].bitcast(I32), 0)
+        nc.vector.memset(z_scales_raw[:].bitcast(I32), 0)
         ident_f32 = keep.tile([P, P], F32)
         make_identity(nc, ident_f32[:])
 
         q_sb = [keep.tile([P, 2, H], BF16, name="q_sb%d" % c) for c in range(B_TILES)]
         hi_sb = [keep.tile([P, T, H], BF16, name="hi_sb%d" % c) for c in range(B_TILES)]
 
-        def load_batch_tile(c):
-            rows = slice(c * P, (c + 1) * P)
-            nc.sync.dma_start(out=q_sb[c][:, 0, :], in_=ht[rows])
-            nc.sync.dma_start(out=q_sb[c][:, 1, :], in_=ct[rows])
-            for t0, t1 in STEP_GROUPS:
-                nc.sync.dma_start(out=hi_sb[c][:, t0:t1, :], in_=hi[rows, t0:t1, :])
+        def load_q(c):
+            nc.sync.dma_start(out=q_sb[c][:, 0, :], in_=ht[c * P : (c + 1) * P])
+            nc.sync.dma_start(out=q_sb[c][:, 1, :], in_=ct[c * P : (c + 1) * P])
 
-        load_batch_tile(0)
-        load_scale_rows(nc, w_planes_raw, PLANE_W_AS[0], W_as_scales)
-        load_scale_rows(nc, w_planes_raw, PLANE_W_AH, W_ah_scales)
-        load_scale_rows(nc, w_planes_raw, PLANE_W_A, W_a_scales)
+        def load_hi(queue, c, t0, t1):
+            queue.dma_start(out=hi_sb[c][:, t0:t1, :], in_=hi[c * P : (c + 1) * P, t0:t1, :])
+
+        bias = keep.tile([P, PACK], BF16)
         w_raw = keep.tile([P, 4, A], U32, align_bytes=64)
         w = keep.tile([P, 4, A], U32, align_bytes=64)
-        w_planes = keep.tile([P, A], U8, align_bytes=64)
-        load_words(nc, w_raw[:, 0, :], W_as_words[0])
-        load_words(nc, w_raw[:, 1, :], W_as_words[1])
-        load_words(nc, w_raw[:, 2, :], W_ah_words[0])
-        bias = keep.tile([P, PACK], BF16)
+        g_scales = keep.tile([P, A], U8, align_bytes=64)
+        z_scales = keep.tile([P, A], U8, align_bytes=64)
+        load_q(0)
+        load_hi(nc.sync, 0, 0, 3)
+        load_scale_rows(nc, g_scales_raw, PLANE_W_AS[0], W_as_scales)
+        load_words(nc, w_raw[:, 0:2, :], W_as_words)
+        load_hi(nc.gpsimd, 0, 3, 5)
+        load_scale_rows(nc, g_scales_raw, PLANE_W_AH, W_ah_scales)
+        load_words(nc, w_raw[:, 2:3, :], W_ah_words)
         nc.sync.dma_start(out=bias[:], in_=ba.rearrange("o (p j) -> (o p) j", j=PACK))
-        load_batch_tile(1)
-        load_words(nc, w_raw[:, 3, :], W_a_words[0])
+        load_q(1)
+        load_hi(nc.gpsimd, 1, 0, 2)
+        load_words(nc, w_raw[:, 3:4, :], W_a_words)
+        load_hi(nc.gpsimd, 1, 2, 5)
+        load_scale_rows(nc, z_scales_raw, PLANE_W_A, W_a_scales)
 
         q_t = [keep.tile([P, 2, P, PACK], BF16, name="q_t%d" % c, align_bytes=64) for c in range(B_TILES)]
         hi_t = [keep.tile([P, T, P, PACK], BF16, name="hi_t%d" % c, align_bytes=64) for c in range(B_TILES)]
@@ -137,18 +144,18 @@ def tile_haint_attention_kernel(
             quantise(q_codes[c][:], q_planes[c][:], q_t[c][:])
 
         def turn_hi(c, s, copy_out):
-            t0, t1 = STEP_GROUPS[s]
+            t0, t1 = STEP_GROUPS[c][s]
             turn(hi_sb[c][:, t0:t1, :], hi_t[c][:, t0:t1], copy_out)
 
         def quantise_hi(c, s):
-            t0, t1 = STEP_GROUPS[s]
+            t0, t1 = STEP_GROUPS[c][s]
             quantise(hi_codes[c][:, t0:t1, :], hi_planes[c][:, t0:t1, :], hi_t[c][:, t0:t1])
 
         flat_g = {}
         grouped_g = {}
 
         def first_stage(c, s):
-            t0, t1 = STEP_GROUPS[s]
+            t0, t1 = STEP_GROUPS[c][s]
             n = t1 - t0
             blocks_per_bank = PACK // n
             flat = stage.tile([P, PACK, n, P], BF16, tag="flat")
@@ -166,7 +173,7 @@ def tile_haint_attention_kernel(
                             nc.tensor.matmul_mx(
                                 out=pre[:, j - j0, t - t0, :],
                                 lhsT=w[:, k, cols].bitcast(FP8X4),
-                                lhsT_scale=w_planes[first_row:P, cols],
+                                lhsT_scale=g_scales[first_row:P, cols],
                                 rhs=codes.bitcast(FP8X4),
                                 rhs_scale=planes,
                                 start=(k == 0),
@@ -178,14 +185,20 @@ def tile_haint_attention_kernel(
                     )
             flat_g[c, s] = flat
 
-        def group_g(c, s):
-            t0, t1 = STEP_GROUPS[s]
+        def group_g(engine, c, s):
+            t0, t1 = STEP_GROUPS[c][s]
             grouped = stage.tile([P, t1 - t0, P, PACK], BF16, tag="grouped", align_bytes=64)
-            nc.vector.tensor_copy(out=grouped[:], in_=flat_g[c, s][:].rearrange("p j i r -> p i r j"))
+            flat = flat_g[c, s][:].rearrange("p j i r -> p i r j")
+            if engine is nc.vector:
+                nc.vector.tensor_copy(out=grouped[:], in_=flat)
+            else:
+                nc.gpsimd.tensor_scalar(
+                    out=grouped[:], in0=flat, scalar1=1.0, scalar2=0.0, op0=ALU.mult, op1=ALU.add
+                )
             grouped_g[c, s] = grouped
 
         def quantise_g(c, s):
-            t0, t1 = STEP_GROUPS[s]
+            t0, t1 = STEP_GROUPS[c][s]
             quantise(g_codes[c][:, t0:t1, :], g_planes[c][:, t0:t1, :], grouped_g[c, s][:])
 
         z = {}
@@ -199,7 +212,7 @@ def tile_haint_attention_kernel(
                 nc.tensor.matmul_mx(
                     out=z_t[:, j, :],
                     lhsT=w[:, 3, cols].bitcast(FP8X4),
-                    lhsT_scale=w_planes[PLANE_W_A:P, cols],
+                    lhsT_scale=z_scales[PLANE_W_A:P, cols],
                     rhs=g_codes[c][:, t, :].bitcast(FP8X4),
                     rhs_scale=g_planes[c][:, t, :],
                     start=True,
@@ -209,12 +222,20 @@ def tile_haint_attention_kernel(
             if t == 0:
                 nc.scalar.copy(out=top[c][:], in_=z_t[:])
 
-        def raise_maximum(c, t):
-            nc.vector.tensor_max(out=top[c][:], in0=top[c][:], in1=z[c, t][:])
+        def raise_maximum(c, t, js=slice(0, PACK)):
+            nc.vector.tensor_max(out=top[c][:, js], in0=top[c][:, js], in1=z[c, t][:, js])
 
-        def shifted_exp(c, t):
-            nc.vector.tensor_sub(out=terms[c][:, 0, t], in0=z[c, t][:], in1=top[c][:])
-            nc.scalar.activation(out=terms[c][:, 0, t], in_=terms[c][:, 0, t], func=ACT.Exp)
+        def shifted_exp(c, t, js=slice(0, PACK)):
+            e = terms[c][:, 0, t, js]
+            nc.vector.tensor_sub(out=e, in0=z[c, t][:, js], in1=top[c][:, js])
+            nc.scalar.activation(out=e, in_=e, func=ACT.Exp)
+
+        def weigh(engine, c, ts, js):
+            engine.tensor_mul(
+                out=terms[c][:, 1, ts, js],
+                in0=terms[c][:, 0, ts, js],
+                in1=hi_t[c][:, ts].rearrange("p t r j -> p t j r")[:, :, js],
+            )
 
         def sum_over_t(total, c, kind, j):
             for t in range(T):
@@ -227,105 +248,128 @@ def tile_haint_attention_kernel(
                     stop=(t == T - 1),
                 )
 
-        def divide_and_store(c, e_total, weighted_total):
-            inverse = stage.tile([P, P, PACK], F32, tag="inverse", bufs=2)
+        inverse = [keep.tile([P, P, PACK], F32, name="inverse%d" % c) for c in range(B_TILES)]
+
+        def square(c, e_total, m0, m1):
             nc.scalar.activation(
-                out=inverse[:], in_=e_total[:].rearrange("p j m -> p m j"), func=ACT.Abs_reciprocal_sqrt
+                out=inverse[c][:, m0:m1], in_=e_total[:].rearrange("p j m -> p m j")[:, m0:m1], func=ACT.Square
             )
-            nc.scalar.activation(out=inverse[:], in_=inverse[:], func=ACT.Square)
-            pooled = stage.tile([P, P, PACK], F32, tag="pooled", bufs=2)
-            nc.vector.tensor_mul(out=pooled[:], in0=weighted_total[:].rearrange("p j m -> p m j"), in1=inverse[:])
-            nc.sync.dma_start(out=out[c * P : (c + 1) * P, :], in_=pooled[:].rearrange("p m j -> p (m j)"))
+
+        def invert(c, m0, m1):
+            nc.scalar.activation(out=inverse[c][:, m0:m1], in_=inverse[c][:, m0:m1], func=ACT.Abs_reciprocal_sqrt)
+
+        def divide_and_store(c, weighted_total, m0, m1):
+            pooled = stage.tile([P, m1 - m0, PACK], F32, tag="pooled", bufs=3)
+            nc.vector.tensor_mul(
+                out=pooled[:],
+                in0=weighted_total[:].rearrange("p j m -> p m j")[:, m0:m1],
+                in1=inverse[c][:, m0:m1],
+            )
+            nc.sync.dma_start(
+                out=out[c * P : (c + 1) * P, PACK * m0 : PACK * m1], in_=pooled[:].rearrange("p m j -> p (m j)")
+            )
 
         vector_copy, scalar_copy = nc.vector.tensor_copy, nc.scalar.copy
 
-        turn_q(0, vector_copy)
-        turn_hi(0, 0, scalar_copy)
-        quantise_q(0)
-        turn_hi(0, 1, vector_copy)
-        quantise_hi(0, 0)
-        turn_hi(0, 2, scalar_copy)
-        quantise_hi(0, 1)
-        regroup(nc, w_planes[:], w_planes_raw[:])
-        quantise_hi(0, 2)
-        for k in range(3):
-            regroup(nc, w[:, k, :].bitcast(I32), w_raw[:, k, :].bitcast(I32))
-
-        first_stage(0, 0)
-        turn_q(1, scalar_copy)
-        first_stage(0, 1)
-        group_g(0, 0)
-        quantise_q(1)
-        turn_hi(1, 0, scalar_copy)
-        first_stage(0, 2)
-        group_g(0, 1)
-        quantise_g(0, 0)
-        turn_hi(1, 1, scalar_copy)
-        quantise_hi(1, 0)
-        regroup(nc, w[:, 3, :].bitcast(I32), w_raw[:, 3, :].bitcast(I32))
-        turn_hi(1, 2, scalar_copy)
-        group_g(0, 2)
-        quantise_g(0, 1)
-        quantise_hi(1, 1)
-        scores(0, 0)
-        scores(0, 1)
-        quantise_g(0, 2)
-        quantise_hi(1, 2)
-        first_stage(1, 0)
-        scores(0, 2)
-        scores(0, 3)
-        raise_maximum(0, 1)
-        raise_maximum(0, 2)
-        scores(0, 4)
-        raise_maximum(0, 3)
-        group_g(1, 0)
-        first_stage(1, 1)
-        raise_maximum(0, 4)
-        quantise_g(1, 0)
-        shifted_exp(0, 0)
-        first_stage(1, 2)
-        shifted_exp(0, 1)
-        group_g(1, 1)
-        scores(1, 0)
-        shifted_exp(0, 2)
-        quantise_g(1, 1)
-        scores(1, 1)
-        shifted_exp(0, 3)
-        group_g(1, 2)
-        scores(1, 2)
-        shifted_exp(0, 4)
-        quantise_g(1, 2)
-        scores(1, 3)
-        for t in range(T):
-            nc.gpsimd.tensor_mul(
-                out=terms[0][:, 1, t], in0=terms[0][:, 0, t], in1=hi_t[0][:, t].rearrange("p r j -> p j r")
-            )
-        raise_maximum(1, 1)
-        scores(1, 4)
-        for t in range(2, T):
-            raise_maximum(1, t)
-        with tc.manual_schedule(engines={mybir.EngineType.Activation}):
+        with tc.manual_schedule(engines={mybir.EngineType.PE}):
+            low, high = slice(0, 2), slice(2, 4)
+            turn_q(0, vector_copy)
+            turn_hi(0, 0, scalar_copy)
+            quantise_q(0)
+            turn_hi(0, 1, scalar_copy)
+            quantise_hi(0, 0)
+            regroup(nc, w[:, 0, :].bitcast(I32), w_raw[:, 0, :].bitcast(I32))
+            regroup(nc, g_scales[:], g_scales_raw[:])
+            regroup(nc, w[:, 1, :].bitcast(I32), w_raw[:, 1, :].bitcast(I32))
+            quantise_hi(0, 1)
+            regroup(nc, w[:, 2, :].bitcast(I32), w_raw[:, 2, :].bitcast(I32))
+            turn_hi(0, 2, vector_copy)
+            first_stage(0, 0)
+            quantise_hi(0, 2)
+            first_stage(0, 1)
+            group_g(nc.vector, 0, 0)
+            quantise_g(0, 0)
+            first_stage(0, 2)
+            group_g(nc.vector, 0, 1)
+            regroup(nc, w[:, 3, :].bitcast(I32), w_raw[:, 3, :].bitcast(I32))
+            quantise_g(0, 1)
+            regroup(nc, z_scales[:], z_scales_raw[:])
+            turn_q(1, vector_copy)
+            turn_hi(1, 0, scalar_copy)
+            turn_hi(1, 1, scalar_copy)
+            group_g(nc.vector, 0, 2)
+            turn_hi(1, 2, scalar_copy)
+            quantise_q(1)
+            scores(0, 0)
+            quantise_g(0, 2)
+            quantise_hi(1, 0)
+            scores(0, 1)
+            scores(0, 2)
+            scores(0, 3)
+            scores(0, 4)
+            for t in (1, 2):
+                for js in (low, high):
+                    raise_maximum(0, t, js)
+            quantise_hi(1, 1)
+            quantise_hi(1, 2)
+            first_stage(1, 0)
+            for t in (3, 4):
+                for js in (low, high):
+                    raise_maximum(0, t, js)
+            first_stage(1, 1)
+            group_g(nc.vector, 1, 0)
+            first_stage(1, 2)
+            quantise_g(1, 0)
+            shifted_exp(0, 0)
+            group_g(nc.vector, 1, 1)
+            shifted_exp(0, 1)
+            quantise_g(1, 1)
+            group_g(nc.vector, 1, 2)
+            scores(1, 0)
+            scores(1, 1)
+            shifted_exp(0, 2)
+            quantise_g(1, 2)
+            scores(1, 2)
+            shifted_exp(0, 3)
+            scores(1, 3)
+            shifted_exp(0, 4)
+            scores(1, 4)
             for t in range(T):
-                shifted_exp(1, t)
+                weigh(nc.gpsimd, 0, slice(t, t + 1), slice(0, PACK))
+            for t in range(1, T):
+                for js in (low, high):
+                    raise_maximum(1, t, js)
+            for t in range(T):
+                shifted_exp(1, t, low)
             e_total_0 = pre_pool.tile([P, PACK, P], F32, tag="pre")
             weighted_total_0 = pre_pool.tile([P, PACK, P], F32, tag="pre")
             e_total_1 = pre_pool.tile([P, PACK, P], F32, tag="pre")
+            weighted_total_1 = sums.tile([P, PACK, P], F32, tag="sums0")
             for j in range(PACK):
                 sum_over_t(e_total_0, 0, 0, j)
+            square(0, e_total_0, 0, P)
+            for t in range(T):
+                shifted_exp(1, t, high)
+            for t in range(3):
+                weigh(nc.gpsimd, 1, slice(t, t + 1), low)
+            weigh(nc.vector, 1, slice(3, T), low)
+            for j in range(0, 2):
+                sum_over_t(e_total_1, 1, 0, j)
             for j in range(PACK):
                 sum_over_t(weighted_total_0, 0, 1, j)
+            weigh(nc.vector, 1, slice(0, T), slice(2, 3))
+            weigh(nc.vector, 1, slice(0, T), slice(3, 4))
+            with tc.manual_schedule(engines={mybir.EngineType.PE, mybir.EngineType.Activation}):
+                invert(0, 0, P)
+                for j in range(2, 4):
+                    sum_over_t(e_total_1, 1, 0, j)
+                half = P // 2
+                for m0 in (0, half):
+                    square(1, e_total_1, m0, m0 + half)
+                for m0 in (0, half):
+                    invert(1, m0, m0 + half)
             for j in range(PACK):
-                sum_over_t(e_total_1, 1, 0, j)
-            weighted_total_1 = sums.tile([P, PACK, P], F32, tag="sums0")
-            for j0 in range(0, PACK, 2):
-                js = slice(j0, j0 + 2)
-                nc.vector.tensor_mul(
-                    out=terms[1][:, 1, :, js],
-                    in0=terms[1][:, 0, :, js],
-                    in1=hi_t[1][:].rearrange("p t r j -> p t j r")[:, :, js],
-                )
-                for j in range(j0, j0 + 2):
-                    sum_over_t(weighted_total_1, 1, 1, j)
-                if j0 == 0:
-                    divide_and_store(0, e_total_0, weighted_total_0)
-            divide_and_store(1, e_total_1, weighted_total_1)
+                sum_over_t(weighted_total_1, 1, 1, j)
+            divide_and_store(0, weighted_total_0, 0, P)
+            for m0 in (0, half):
+                divide_and_store(1, weighted_total_1, m0, m0 + half)

@@ -44,7 +44,8 @@ def load_words(nc, words_sb, words):
 
 def regroup(nc, out, in_):
     nc.vector.tensor_copy(
-        out=out.rearrange("p (j m) -> p j m", j=PACK), in_=in_.rearrange("p (m j) -> p j m", j=PACK)
+        out=out.rearrange("p (j b i) -> p b j i", j=PACK, i=4),
+        in_=in_.rearrange("p (b i j) -> p b j i", j=PACK, i=4),
     )
 
 
@@ -79,6 +80,25 @@ def tile_haint_attention_kernel(
         nc.vector.memset(z_scales_raw[:].bitcast(I32), 0)
         ident_f32 = keep.tile([P, P], F32)
         make_identity(nc, ident_f32[:])
+
+        zeros = keep.tile([P, 512], BF16)
+        nc.vector.memset(zeros[:], 0.0)
+
+        def keep_clock(bank):
+            nc.tensor.matmul(
+                out=bank.rearrange("p i r -> p (i r)"), lhsT=zeros[:, 0:P], rhs=zeros[:], start=True, stop=True
+            )
+
+        def keep_clock_mx(bank):
+            nc.tensor.matmul_mx(
+                out=bank.rearrange("p i r -> p (i r)"),
+                lhsT=w[:, 3, 0:P].bitcast(FP8X4),
+                lhsT_scale=z_scales[PLANE_W_A:P, 0:P],
+                rhs=g_codes[0][:, 0:4, :].rearrange("p i r -> p (i r)").bitcast(FP8X4),
+                rhs_scale=g_planes[0][:, 0:4, :].rearrange("p i r -> p (i r)"),
+                start=True,
+                stop=True,
+            )
 
         q_sb = [keep.tile([P, 2, H], BF16, name="q_sb%d" % c) for c in range(B_TILES)]
         hi_sb = [keep.tile([P, T, H], BF16, name="hi_sb%d" % c) for c in range(B_TILES)]
@@ -188,9 +208,11 @@ def tile_haint_attention_kernel(
         def group_g(engine, c, s):
             t0, t1 = STEP_GROUPS[c][s]
             grouped = stage.tile([P, t1 - t0, P, PACK], BF16, tag="grouped", align_bytes=64)
-            flat = flat_g[c, s][:].rearrange("p j i r -> p i r j")
+            flat = flat_g[c, s][:].rearrange("p j i r -> p j (i r)").rearrange("p j (b q) -> p b j q", q=4)
             if engine is nc.vector:
-                nc.vector.tensor_copy(out=grouped[:], in_=flat)
+                nc.vector.tensor_copy(
+                    out=grouped[:].rearrange("p i r j -> p (i r) j").rearrange("p (b q) j -> p b j q", q=4), in_=flat
+                )
             else:
                 nc.gpsimd.tensor_scalar(
                     out=grouped[:], in0=flat, scalar1=1.0, scalar2=0.0, op0=ALU.mult, op1=ALU.add
@@ -273,10 +295,16 @@ def tile_haint_attention_kernel(
 
         with tc.manual_schedule(engines={mybir.EngineType.PE}):
             low, high = slice(0, 2), slice(2, 4)
+            warm_bank = sums.tile([P, PACK, P], F32, tag="sums0")
+            for k in range(4):
+                keep_clock(warm_bank[:])
             turn_q(0, vector_copy)
+            keep_clock(warm_bank[:])
             turn_hi(0, 0, scalar_copy)
             quantise_q(0)
             turn_hi(0, 1, scalar_copy)
+            for k in range(2):
+                keep_clock(warm_bank[:])
             quantise_hi(0, 0)
             regroup(nc, w[:, 0, :].bitcast(I32), w_raw[:, 0, :].bitcast(I32))
             regroup(nc, g_scales[:], g_scales_raw[:])
@@ -347,6 +375,8 @@ def tile_haint_attention_kernel(
             weighted_total_1 = sums.tile([P, PACK, P], F32, tag="sums0")
             for j in range(PACK):
                 sum_over_t(e_total_0, 0, 0, j)
+            for k in range(4):
+                keep_clock_mx(weighted_total_0[:])
             square(0, e_total_0, 0, P)
             for t in range(T):
                 shifted_exp(1, t, high)

@@ -208,14 +208,19 @@ def tile_haint_attention_kernel(
         def group_g(engine, c, s):
             t0, t1 = STEP_GROUPS[c][s]
             grouped = stage.tile([P, t1 - t0, P, PACK], BF16, tag="grouped", align_bytes=64)
-            flat = flat_g[c, s][:].rearrange("p j i r -> p j (i r)").rearrange("p j (b q) -> p b j q", q=4)
             if engine is nc.vector:
                 nc.vector.tensor_copy(
-                    out=grouped[:].rearrange("p i r j -> p (i r) j").rearrange("p (b q) j -> p b j q", q=4), in_=flat
+                    out=grouped[:].rearrange("p i r j -> p (i r) j").rearrange("p (b q) j -> p b j q", q=4),
+                    in_=flat_g[c, s][:].rearrange("p j i r -> p j (i r)").rearrange("p j (b q) -> p b j q", q=4),
                 )
             else:
                 nc.gpsimd.tensor_scalar(
-                    out=grouped[:], in0=flat, scalar1=1.0, scalar2=0.0, op0=ALU.mult, op1=ALU.add
+                    out=grouped[:],
+                    in0=flat_g[c, s][:].rearrange("p j i r -> p i r j"),
+                    scalar1=1.0,
+                    scalar2=0.0,
+                    op0=ALU.mult,
+                    op1=ALU.add,
                 )
             grouped_g[c, s] = grouped
 
@@ -296,33 +301,35 @@ def tile_haint_attention_kernel(
         with tc.manual_schedule(engines={mybir.EngineType.PE}):
             low, high = slice(0, 2), slice(2, 4)
             warm_bank = sums.tile([P, PACK, P], F32, tag="sums0")
-            for k in range(4):
-                keep_clock(warm_bank[:])
-            turn_q(0, vector_copy)
-            keep_clock(warm_bank[:])
-            turn_hi(0, 0, scalar_copy)
-            quantise_q(0)
-            turn_hi(0, 1, scalar_copy)
             for k in range(2):
                 keep_clock(warm_bank[:])
-            quantise_hi(0, 0)
-            regroup(nc, w[:, 0, :].bitcast(I32), w_raw[:, 0, :].bitcast(I32))
-            regroup(nc, g_scales[:], g_scales_raw[:])
-            regroup(nc, w[:, 1, :].bitcast(I32), w_raw[:, 1, :].bitcast(I32))
-            quantise_hi(0, 1)
-            regroup(nc, w[:, 2, :].bitcast(I32), w_raw[:, 2, :].bitcast(I32))
-            turn_hi(0, 2, vector_copy)
-            first_stage(0, 0)
-            quantise_hi(0, 2)
-            first_stage(0, 1)
-            group_g(nc.vector, 0, 0)
-            quantise_g(0, 0)
-            first_stage(0, 2)
-            group_g(nc.vector, 0, 1)
-            regroup(nc, w[:, 3, :].bitcast(I32), w_raw[:, 3, :].bitcast(I32))
+            with tc.manual_schedule(engines={mybir.EngineType.PE, mybir.EngineType.DVE}):
+                turn_q(0, vector_copy)
+                for k in range(2):
+                    keep_clock(warm_bank[:])
+                quantise_q(0)
+                turn_hi(0, 0, scalar_copy)
+                turn_hi(0, 1, scalar_copy)
+                for k in range(3):
+                    keep_clock(warm_bank[:])
+                for k in range(2):
+                    regroup(nc, w[:, k, :].bitcast(I32), w_raw[:, k, :].bitcast(I32))
+                quantise_hi(0, 0)
+                regroup(nc, g_scales[:], g_scales_raw[:])
+                quantise_hi(0, 1)
+                regroup(nc, w[:, 2, :].bitcast(I32), w_raw[:, 2, :].bitcast(I32))
+                turn_hi(0, 2, scalar_copy)
+                first_stage(0, 0)
+                quantise_hi(0, 2)
+                first_stage(0, 1)
+                group_g(nc.vector, 0, 0)
+                regroup(nc, w[:, 3, :].bitcast(I32), w_raw[:, 3, :].bitcast(I32))
+                quantise_g(0, 0)
+                first_stage(0, 2)
+                regroup(nc, z_scales[:], z_scales_raw[:])
+                group_g(nc.vector, 0, 1)
+            turn_q(1, scalar_copy)
             quantise_g(0, 1)
-            regroup(nc, z_scales[:], z_scales_raw[:])
-            turn_q(1, vector_copy)
             turn_hi(1, 0, scalar_copy)
             turn_hi(1, 1, scalar_copy)
             group_g(nc.vector, 0, 2)
@@ -331,10 +338,8 @@ def tile_haint_attention_kernel(
             scores(0, 0)
             quantise_g(0, 2)
             quantise_hi(1, 0)
-            scores(0, 1)
-            scores(0, 2)
-            scores(0, 3)
-            scores(0, 4)
+            for t in range(1, T):
+                scores(0, t)
             for t in (1, 2):
                 for js in (low, high):
                     raise_maximum(0, t, js)
@@ -345,7 +350,7 @@ def tile_haint_attention_kernel(
                 for js in (low, high):
                     raise_maximum(0, t, js)
             first_stage(1, 1)
-            group_g(nc.vector, 1, 0)
+            group_g(nc.gpsimd, 1, 0)
             first_stage(1, 2)
             quantise_g(1, 0)
             shifted_exp(0, 0)
@@ -364,10 +369,13 @@ def tile_haint_attention_kernel(
             scores(1, 4)
             for t in range(T):
                 weigh(nc.gpsimd, 0, slice(t, t + 1), slice(0, PACK))
-            for t in range(1, T):
+            for t in range(1, T - 1):
                 for js in (low, high):
                     raise_maximum(1, t, js)
-            for t in range(T):
+            raise_maximum(1, T - 1, low)
+            shifted_exp(1, 0, low)
+            raise_maximum(1, T - 1, high)
+            for t in range(1, T):
                 shifted_exp(1, t, low)
             e_total_0 = pre_pool.tile([P, PACK, P], F32, tag="pre")
             weighted_total_0 = pre_pool.tile([P, PACK, P], F32, tag="pre")
@@ -380,13 +388,13 @@ def tile_haint_attention_kernel(
             square(0, e_total_0, 0, P)
             for t in range(T):
                 shifted_exp(1, t, high)
-            for t in range(3):
+            for t in range(2):
                 weigh(nc.gpsimd, 1, slice(t, t + 1), low)
-            weigh(nc.vector, 1, slice(3, T), low)
-            for j in range(0, 2):
-                sum_over_t(e_total_1, 1, 0, j)
+            weigh(nc.vector, 1, slice(2, T), low)
             for j in range(PACK):
                 sum_over_t(weighted_total_0, 0, 1, j)
+            for j in range(0, 2):
+                sum_over_t(e_total_1, 1, 0, j)
             weigh(nc.vector, 1, slice(0, T), slice(2, 3))
             weigh(nc.vector, 1, slice(0, T), slice(3, 4))
             with tc.manual_schedule(engines={mybir.EngineType.PE, mybir.EngineType.Activation}):

from contextlib import ExitStack

import concourse.mybir as mybir
from concourse.masks import make_identity

F32 = mybir.dt.float32
BF16 = mybir.dt.bfloat16
I32 = mybir.dt.int32
U32 = mybir.dt.uint32
U8 = mybir.dt.uint8
FP8X4 = mybir.dt.float8_e4m3fn_x4
ACT = mybir.ActivationFunctionType
ALU = mybir.AluOpType

P = 128
PACK = 4
B, T, H, A = 256, 5, 512, 512
B_TILES = B // P
STEP_GROUPS = (((0, 1), (1, 3), (3, 5)), ((0, 2), (2, 4), (4, 5)))

PLANE_W_AS = (0, 4)
PLANE_W_AH = 8
PLANE_W_A = 0

FLOPS = 2 * B * (2 * H) * A + 2 * B * T * H * A + 2 * B * T * A * H


def load_scale_rows(nc, w_planes, first_row, scales):
    n_planes = scales.shape[0]
    for quadrant in range(4):
        first = 32 * quadrant + first_row
        nc.sync.dma_start(
            out=w_planes[first : first + 4 * n_planes, :].bitcast(I32),
            in_=scales[:, 4 * quadrant : 4 * quadrant + 4, :].bitcast(I32),
        )


def load_words(nc, words_sb, words):
    nc.sync.dma_start(
        out=words_sb.bitcast(I32),
        in_=words.rearrange("g p n t -> p g (n t)").bitcast(I32),
    )


def regroup(nc, out, in_):
    nc.vector.tensor_copy(
        out=out.rearrange("p (j b i) -> p b j i", j=PACK, i=4),
        in_=in_.rearrange("p (b i j) -> p b j i", j=PACK, i=4),
    )


def tile_haint_attention_kernel(
    tc,
    ht,
    ct,
    hi,
    W_as_words,
    W_as_scales,
    W_ah_words,
    W_ah_scales,
    ba,
    v,
    W_a_words,
    W_a_scales,
    out,
):
    nc = tc.nc
    with ExitStack() as ctx:
        keep = ctx.enter_context(tc.tile_pool(name="keep", bufs=1))
        stage = ctx.enter_context(tc.tile_pool(name="stage", bufs=3))
        pre_pool = ctx.enter_context(tc.psum_pool(name="pre_pool", bufs=3))
        sums = ctx.enter_context(tc.psum_pool(name="sums", bufs=1))

        warm = keep.tile([P, 1], F32)
        nc.vector.memset(warm[:], 0.0)
        nc.scalar.activation(out=warm[:], in_=warm[:], func=ACT.Tanh)
        g_scales_raw = keep.tile([P, A], U8, align_bytes=64)
        z_scales_raw = keep.tile([P, A], U8, align_bytes=64)
        nc.vector.memset(g_scales_raw[:].bitcast(I32), 0)
        nc.vector.memset(z_scales_raw[:].bitcast(I32), 0)
        ident_f32 = keep.tile([P, P], F32)
        make_identity(nc, ident_f32[:])

        zeros = keep.tile([P, 512], BF16)
        nc.vector.memset(zeros[:], 0.0)

        def keep_clock(bank):
            nc.tensor.matmul(
                out=bank.rearrange("p i r -> p (i r)"), lhsT=zeros[:, 0:P], rhs=zeros[:], start=True, stop=True
            )

        def keep_clock_mx(bank):
            nc.tensor.matmul_mx(
                out=bank.rearrange("p i r -> p (i r)"),
                lhsT=w[:, 3, 0:P].bitcast(FP8X4),
                lhsT_scale=z_scales[PLANE_W_A:P, 0:P],
                rhs=g_codes[0][:, 0:4, :].rearrange("p i r -> p (i r)").bitcast(FP8X4),
                rhs_scale=g_planes[0][:, 0:4, :].rearrange("p i r -> p (i r)"),
                start=True,
                stop=True,
            )

        q_sb = [keep.tile([P, 2, H], BF16, name="q_sb%d" % c) for c in range(B_TILES)]
        hi_sb = [keep.tile([P, T, H], BF16, name="hi_sb%d" % c) for c in range(B_TILES)]

        def load_q(c):
            nc.sync.dma_start(out=q_sb[c][:, 0, :], in_=ht[c * P : (c + 1) * P])
            nc.sync.dma_start(out=q_sb[c][:, 1, :], in_=ct[c * P : (c + 1) * P])

        def load_hi(queue, c, t0, t1):
            queue.dma_start(out=hi_sb[c][:, t0:t1, :], in_=hi[c * P : (c + 1) * P, t0:t1, :])

        bias = keep.tile([P, PACK], BF16)
        w_raw = keep.tile([P, 4, A], U32, align_bytes=64)
        w = keep.tile([P, 4, A], U32, align_bytes=64)
        g_scales = keep.tile([P, A], U8, align_bytes=64)
        z_scales = keep.tile([P, A], U8, align_bytes=64)
        load_q(0)
        load_hi(nc.sync, 0, 0, 3)
        load_scale_rows(nc, g_scales_raw, PLANE_W_AS[0], W_as_scales)
        load_words(nc, w_raw[:, 0:2, :], W_as_words)
        load_hi(nc.gpsimd, 0, 3, 5)
        load_scale_rows(nc, g_scales_raw, PLANE_W_AH, W_ah_scales)
        load_words(nc, w_raw[:, 2:3, :], W_ah_words)
        nc.sync.dma_start(out=bias[:], in_=ba.rearrange("o (p j) -> (o p) j", j=PACK))
        load_q(1)
        load_hi(nc.gpsimd, 1, 0, 2)
        load_words(nc, w_raw[:, 3:4, :], W_a_words)
        load_hi(nc.gpsimd, 1, 2, 5)
        load_scale_rows(nc, z_scales_raw, PLANE_W_A, W_a_scales)

        q_t = [keep.tile([P, 2, P, PACK], BF16, name="q_t%d" % c, align_bytes=64) for c in range(B_TILES)]
        hi_t = [keep.tile([P, T, P, PACK], BF16, name="hi_t%d" % c, align_bytes=64) for c in range(B_TILES)]
        q_codes = [keep.tile([P, 2, P], U32, name="q_codes%d" % c, align_bytes=64) for c in range(B_TILES)]
        q_planes = [keep.tile([P, 2, P], U8, name="q_planes%d" % c, align_bytes=64) for c in range(B_TILES)]
        hi_codes = [keep.tile([P, T, P], U32, name="hi_codes%d" % c, align_bytes=64) for c in range(B_TILES)]
        hi_planes = [keep.tile([P, T, P], U8, name="hi_planes%d" % c, align_bytes=64) for c in range(B_TILES)]
        g_codes = [keep.tile([P, T, P], U32, name="g_codes%d" % c, align_bytes=64) for c in range(B_TILES)]
        g_planes = [keep.tile([P, T, P], U8, name="g_planes%d" % c, align_bytes=64) for c in range(B_TILES)]

        turns = []

        def turn(source, target, copy_out):
            n = source.shape[1]
            words_t = sums.tile([P, 2, 2, P], F32, tag="sums%d" % (2 + len(turns) % 3))
            turns.append(n)
            for i in range(n):
                words = source[:, i, :].bitcast(F32)
                for u in range(2):
                    nc.tensor.transpose(words_t[:, i, u, :], words[:, u : H // 2 : 2], ident_f32[:])
            copy_out(out=target.bitcast(F32), in_=words_t[:, 0:n].rearrange("p i u r -> p i r u"))

        def quantise(codes, planes, grouped):
            nc.vector.quantize_mx(
                out=codes.rearrange("p i r -> p (i r)").bitcast(FP8X4),
                scales=planes.rearrange("p i r -> p (i r)"),
                in_=grouped.rearrange("p i r j -> p (i r j)"),
            )

        def turn_q(c, copy_out):
            turn(q_sb[c][:], q_t[c][:], copy_out)

        def quantise_q(c):
            quantise(q_codes[c][:], q_planes[c][:], q_t[c][:])

        def turn_hi(c, s, copy_out):
            t0, t1 = STEP_GROUPS[c][s]
            turn(hi_sb[c][:, t0:t1, :], hi_t[c][:, t0:t1], copy_out)

        def quantise_hi(c, s):
            t0, t1 = STEP_GROUPS[c][s]
            quantise(hi_codes[c][:, t0:t1, :], hi_planes[c][:, t0:t1, :], hi_t[c][:, t0:t1])

        flat_g = {}
        grouped_g = {}

        def first_stage(c, s):
            t0, t1 = STEP_GROUPS[c][s]
            n = t1 - t0
            blocks_per_bank = PACK // n
            flat = stage.tile([P, PACK, n, P], BF16, tag="flat")
            for j0 in range(0, PACK, blocks_per_bank):
                pre = pre_pool.tile([P, blocks_per_bank, n, P], F32, tag="pre")
                for j in range(j0, j0 + blocks_per_bank):
                    cols = slice(j * P, (j + 1) * P)
                    for t in range(t0, t1):
                        moving = (
                            (q_codes[c][:, 0, :], q_planes[c][:, 0, :], PLANE_W_AS[0]),
                            (q_codes[c][:, 1, :], q_planes[c][:, 1, :], PLANE_W_AS[1]),
                            (hi_codes[c][:, t, :], hi_planes[c][:, t, :], PLANE_W_AH),
                        )
                        for k, (codes, planes, first_row) in enumerate(moving):
                            nc.tensor.matmul_mx(
                                out=pre[:, j - j0, t - t0, :],
                                lhsT=w[:, k, cols].bitcast(FP8X4),
                                lhsT_scale=g_scales[first_row:P, cols],
                                rhs=codes.bitcast(FP8X4),
                                rhs_scale=planes,
                                start=(k == 0),
                                stop=(k == 2),
                            )
                for j in range(j0, j0 + blocks_per_bank):
                    nc.scalar.activation(
                        out=flat[:, j], in_=pre[:, j - j0], func=ACT.Tanh, bias=bias[:, j : j + 1]
                    )
            flat_g[c, s] = flat

        def group_g(engine, c, s):
            t0, t1 = STEP_GROUPS[c][s]
            grouped = stage.tile([P, t1 - t0, P, PACK], BF16, tag="grouped", align_bytes=64)
            if engine is nc.vector:
                nc.vector.tensor_copy(
                    out=grouped[:].rearrange("p i r j -> p (i r) j").rearrange("p (b q) j -> p b j q", q=4),
                    in_=flat_g[c, s][:].rearrange("p j i r -> p j (i r)").rearrange("p j (b q) -> p b j q", q=4),
                )
            else:
                nc.gpsimd.tensor_scalar(
                    out=grouped[:],
                    in0=flat_g[c, s][:].rearrange("p j i r -> p i r j"),
                    scalar1=1.0,
                    scalar2=0.0,
                    op0=ALU.mult,
                    op1=ALU.add,
                )
            grouped_g[c, s] = grouped

        def quantise_g(c, s):
            t0, t1 = STEP_GROUPS[c][s]
            quantise(g_codes[c][:, t0:t1, :], g_planes[c][:, t0:t1, :], grouped_g[c, s][:])

        z = {}
        top = [keep.tile([P, PACK, P], F32, name="top%d" % c) for c in range(B_TILES)]
        terms = [keep.tile([P, 2, T, PACK, P], F32, name="terms%d" % c) for c in range(B_TILES)]

        def scores(c, t):
            z_t = sums.tile([P, PACK, P], F32, tag="sums%d" % t)
            for j in range(PACK):
                cols = slice(j * P, (j + 1) * P)
                nc.tensor.matmul_mx(
                    out=z_t[:, j, :],
                    lhsT=w[:, 3, cols].bitcast(FP8X4),
                    lhsT_scale=z_scales[PLANE_W_A:P, cols],
                    rhs=g_codes[c][:, t, :].bitcast(FP8X4),
                    rhs_scale=g_planes[c][:, t, :],
                    start=True,
                    stop=True,
                )
            z[c, t] = z_t
            if t == 0:
                nc.scalar.copy(out=top[c][:], in_=z_t[:])

        def raise_maximum(c, t, js=slice(0, PACK)):
            nc.vector.tensor_max(out=top[c][:, js], in0=top[c][:, js], in1=z[c, t][:, js])

        def shifted_exp(c, t, js=slice(0, PACK)):
            e = terms[c][:, 0, t, js]
            nc.vector.tensor_sub(out=e, in0=z[c, t][:, js], in1=top[c][:, js])
            nc.scalar.activation(out=e, in_=e, func=ACT.Exp)

        def weigh(engine, c, ts, js):
            engine.tensor_mul(
                out=terms[c][:, 1, ts, js],
                in0=terms[c][:, 0, ts, js],
                in1=hi_t[c][:, ts].rearrange("p t r j -> p t j r")[:, :, js],
            )

        def sum_over_t(total, c, kind, j):
            for t in range(T):
                nc.tensor.matmul(
                    out=total[:, j, :],
                    lhsT=terms[c][:, kind, t, j, :],
                    rhs=ident_f32[:],
                    is_transpose=True,
                    start=(t == 0),
                    stop=(t == T - 1),
                )

        inverse = [keep.tile([P, P, PACK], F32, name="inverse%d" % c) for c in range(B_TILES)]

        def square(c, e_total, m0, m1):
            nc.scalar.activation(
                out=inverse[c][:, m0:m1], in_=e_total[:].rearrange("p j m -> p m j")[:, m0:m1], func=ACT.Square
            )

        def invert(c, m0, m1):
            nc.scalar.activation(out=inverse[c][:, m0:m1], in_=inverse[c][:, m0:m1], func=ACT.Abs_reciprocal_sqrt)

        def divide_and_store(c, weighted_total, m0, m1):
            pooled = stage.tile([P, m1 - m0, PACK], F32, tag="pooled", bufs=3)
            nc.vector.tensor_mul(
                out=pooled[:],
                in0=weighted_total[:].rearrange("p j m -> p m j")[:, m0:m1],
                in1=inverse[c][:, m0:m1],
            )
            nc.sync.dma_start(
                out=out[c * P : (c + 1) * P, PACK * m0 : PACK * m1], in_=pooled[:].rearrange("p m j -> p (m j)")
            )

        vector_copy, scalar_copy = nc.vector.tensor_copy, nc.scalar.copy

        with tc.manual_schedule(engines={mybir.EngineType.PE}):
            low, high = slice(0, 2), slice(2, 4)
            warm_bank = sums.tile([P, PACK, P], F32, tag="sums0")
            for k in range(2):
                keep_clock(warm_bank[:])
            with tc.manual_schedule(engines={mybir.EngineType.PE, mybir.EngineType.DVE}):
                turn_q(0, vector_copy)
                for k in range(2):
                    keep_clock(warm_bank[:])
                quantise_q(0)
                turn_hi(0, 0, scalar_copy)
                turn_hi(0, 1, scalar_copy)
                for k in range(3):
                    keep_clock(warm_bank[:])
                for k in range(2):
                    regroup(nc, w[:, k, :].bitcast(I32), w_raw[:, k, :].bitcast(I32))
                quantise_hi(0, 0)
                regroup(nc, g_scales[:], g_scales_raw[:])
                quantise_hi(0, 1)
                regroup(nc, w[:, 2, :].bitcast(I32), w_raw[:, 2, :].bitcast(I32))
                turn_hi(0, 2, scalar_copy)
                first_stage(0, 0)
                quantise_hi(0, 2)
                first_stage(0, 1)
                group_g(nc.vector, 0, 0)
                regroup(nc, w[:, 3, :].bitcast(I32), w_raw[:, 3, :].bitcast(I32))
                quantise_g(0, 0)
                first_stage(0, 2)
                regroup(nc, z_scales[:], z_scales_raw[:])
                group_g(nc.vector, 0, 1)
            turn_q(1, scalar_copy)
            quantise_g(0, 1)
            turn_hi(1, 0, scalar_copy)
            turn_hi(1, 1, scalar_copy)
            group_g(nc.vector, 0, 2)
            turn_hi(1, 2, scalar_copy)
            quantise_q(1)
            scores(0, 0)
            quantise_g(0, 2)
            quantise_hi(1, 0)
            for t in range(1, T):
                scores(0, t)
            for t in (1, 2):
                for js in (low, high):
                    raise_maximum(0, t, js)
            quantise_hi(1, 1)
            quantise_hi(1, 2)
            first_stage(1, 0)
            for t in (3, 4):
                for js in (low, high):
                    raise_maximum(0, t, js)
            first_stage(1, 1)
            group_g(nc.gpsimd, 1, 0)
            first_stage(1, 2)
            quantise_g(1, 0)
            shifted_exp(0, 0)
            group_g(nc.vector, 1, 1)
            shifted_exp(0, 1)
            quantise_g(1, 1)
            group_g(nc.vector, 1, 2)
            scores(1, 0)
            scores(1, 1)
            shifted_exp(0, 2)
            quantise_g(1, 2)
            scores(1, 2)
            shifted_exp(0, 3)
            scores(1, 3)
            shifted_exp(0, 4)
            scores(1, 4)
            for t in range(T):
                weigh(nc.gpsimd, 0, slice(t, t + 1), slice(0, PACK))
            for t in range(1, T - 1):
                for js in (low, high):
                    raise_maximum(1, t, js)
            raise_maximum(1, T - 1, low)
            shifted_exp(1, 0, low)
            raise_maximum(1, T - 1, high)
            for t in range(1, T):
                shifted_exp(1, t, low)
            e_total_0 = pre_pool.tile([P, PACK, P], F32, tag="pre")
            weighted_total_0 = pre_pool.tile([P, PACK, P], F32, tag="pre")
            e_total_1 = pre_pool.tile([P, PACK, P], F32, tag="pre")
            weighted_total_1 = sums.tile([P, PACK, P], F32, tag="sums0")
            for j in range(PACK):
                sum_over_t(e_total_0, 0, 0, j)
            for k in range(4):
                keep_clock_mx(weighted_total_0[:])
            square(0, e_total_0, 0, P)
            for t in range(T):
                shifted_exp(1, t, high)
            for t in range(2):
                weigh(nc.gpsimd, 1, slice(t, t + 1), low)
            weigh(nc.vector, 1, slice(2, T), low)
            for j in range(PACK):
                sum_over_t(weighted_total_0, 0, 1, j)
            for j in range(0, 2):
                sum_over_t(e_total_1, 1, 0, j)
            weigh(nc.vector, 1, slice(0, T), slice(2, 3))
            weigh(nc.vector, 1, slice(0, T), slice(3, 4))
            with tc.manual_schedule(engines={mybir.EngineType.PE, mybir.EngineType.Activation}):
                invert(0, 0, P)
                for j in range(2, 4):
                    sum_over_t(e_total_1, 1, 0, j)
                half = P // 2
                for m0 in (0, half):
                    square(1, e_total_1, m0, m0 + half)
                for m0 in (0, half):
                    invert(1, m0, m0 + half)
            for j in range(PACK):
                sum_over_t(weighted_total_1, 1, 1, j)
            divide_and_store(0, weighted_total_0, 0, P)
            for m0 in (0, half):
                divide_and_store(1, weighted_total_1, m0, m0 + half)
